import numpy as np
import ml_dtypes


def mxq(x, axis, fmt="e4m3"):
    dtype, down = {"e4m3": (ml_dtypes.float8_e4m3fn, 7), "e5m2": (ml_dtypes.float8_e5m2, 14)}[fmt]
    v = np.moveaxis(np.asarray(x, np.float32).astype(ml_dtypes.bfloat16).astype(np.float64), axis, -1)
    blocks = v.reshape(v.shape[:-1] + (-1, 32))
    amax = np.abs(blocks).max(-1, keepdims=True)
    byte = np.maximum(np.where(amax > 0, np.frexp(amax)[1] - 1 + 127, 0) - down, 1)
    scale = np.exp2(byte - 127.0)
    codes = (blocks / scale).astype(np.float32).astype(dtype).astype(np.float64)
    return np.moveaxis((codes * scale).reshape(v.shape), -1, axis)


WIDE = False


def mx_kscale(k):
    if not WIDE:
        return np.ones(k)
    levels = np.array([10, -10, 5, -5, 0])
    if k % 512:
        return np.exp2(np.random.permutation(np.resize(levels, k // 32))).repeat(32)
    a = np.empty((k // 512, 16))
    for p in range(k // 512):
        a[p, :8] = np.random.permutation(np.resize(levels, 8))
        for g in range(8):
            far = levels[np.abs(levels - a[p, g]) >= 10]
            a[p, g + 8] = far[np.random.randint(len(far))]
    return np.exp2(a.ravel()).repeat(32)


BF16 = ml_dtypes.bfloat16


def bf(x):
    return np.asarray(x, np.float32).astype(BF16)


def f64(x):
    return np.asarray(x).astype(np.float64)


IN, H, C, B = 8192, 512, 2, 128
QH = H % 512 == 0


def sigmoid(v):
    return 1.0 / (1.0 + np.exp(-v))


def setup_inputs():
    s = mx_kscale(IN)
    t = mx_kscale(H) if QH else np.ones(H)
    return {"input_word": bf(np.random.standard_normal((B, IN)) * s),
            "hidden_states": bf(np.random.standard_normal((B, H)) * t),
            "Wx": bf(np.random.uniform(-1.0, 1.0, (C, 2 * H, IN)) / np.sqrt(IN) / s),
            "bx": bf(np.random.standard_normal((C, 2 * H)) * 0.3),
            "Wh": bf(np.random.uniform(-1.0, 1.0, (C, 2 * H, H)) / np.sqrt(H) / t)}


def reference(input_word, hidden_states, Wx, bx, Wh):
    px = mxq(f64(input_word), 1, "e4m3") @ mxq(f64(Wx), 2, "e4m3").transpose(0, 2, 1)
    if QH:
        ph = mxq(f64(hidden_states), 1, "e4m3") @ mxq(f64(Wh), 2, "e4m3").transpose(0, 2, 1)
    else:
        ph = f64(hidden_states) @ f64(Wh).transpose(0, 2, 1)
    net = px.transpose(1, 0, 2) + ph.transpose(1, 0, 2) + f64(bx)[None, :, :]
    input_gate, cell_states = net[..., :H], net[..., H:]
    cell_input = np.tanh(cell_states)
    input_gate = sigmoid(input_gate)
    return (cell_input, input_gate)

@@ -1,0 +1,237 @@
+from contextlib import ExitStack
+
+import concourse.masks as masks
+import concourse.mybir as mybir
+
+F32 = mybir.dt.float32
+BF16 = mybir.dt.bfloat16
+I32 = mybir.dt.int32
+U32 = mybir.dt.uint32
+U8 = mybir.dt.uint8
+FP8X4 = mybir.dt.float8_e4m3fn_x4
+ACT = mybir.ActivationFunctionType
+ALU = mybir.AluOpType
+
+P = 128
+PACK = 4
+K_PASS = P * PACK
+IN = 8192
+H = 512
+CELLS = 2
+GATES = 2
+OUT = CELLS * GATES * H
+X_PASSES = IN // K_PASS
+BLOCKS = OUT // P
+BLOCKS_PER_GATE = H // P
+
+WORDS_PER_PASS = K_PASS // 2
+BANK_WORDS = 512
+PASSES_PER_BANK = BANK_WORDS // WORDS_PER_PASS
+UNIT_BANKS = X_PASSES // PASSES_PER_BANK
+UNIT_LOADS = 2
+LOAD_PASSES = X_PASSES // UNIT_LOADS
+X_LOADS = 4
+
+QUANTISE_LAG = 2
+VECTOR_COPY_EVERY = 4
+
+RAW_UNITS = 6
+TRANSPOSE_BANKS = 6
+SUM_BANKS = 2
+
+FLOPS = 2 * P * OUT * (IN + H)
+
+
+def tile_compute_gate_k_kernel(tc, input_word, hidden_states, Wx, bx, Wh, out_0, out_1):
+    nc = tc.nc
+    with ExitStack() as ctx:
+        keep = ctx.enter_context(tc.tile_pool(name="keep", bufs=1))
+        raw_pool = ctx.enter_context(tc.tile_pool(name="raw", bufs=RAW_UNITS * UNIT_LOADS))
+        grouped_pool = ctx.enter_context(tc.tile_pool(name="grouped", bufs=QUANTISE_LAG + 4))
+        weight_pool = ctx.enter_context(tc.tile_pool(name="weight", bufs=3))
+        out_pool = ctx.enter_context(tc.tile_pool(name="out", bufs=3))
+        banks = ctx.enter_context(tc.psum_pool(name="banks", bufs=TRANSPOSE_BANKS))
+        sums = ctx.enter_context(tc.psum_pool(name="sums", bufs=SUM_BANKS))
+        ctx.enter_context(tc.manual_schedule())
+
+        def load_unit(rows):
+            parts = []
+            for part in range(UNIT_LOADS):
+                raw = raw_pool.tile([P, LOAD_PASSES * K_PASS], BF16, name="raw")
+                nc.sync.dma_start(
+                    out=raw[:].rearrange("p (g k) -> p g k", k=K_PASS),
+                    in_=rows[:, part * LOAD_PASSES : (part + 1) * LOAD_PASSES, :],
+                )
+                parts.append(raw)
+            return parts
+
+        copied = []
+
+        def quantise(n):
+            grouped, codes, scales = copied[n]
+            nc.vector.quantize_mx(out=codes.bitcast(FP8X4), scales=scales, in_=grouped[:])
+
+        def transpose_bank(words, passes, codes, scales):
+            bank = banks.tile([P, BANK_WORDS], F32, name="bank")
+            for g in range(passes):
+                for u in range(2):
+                    first = (2 * g + u) * P
+                    every_2nd = words[:, 2 * g * P + u : 2 * (g + 1) * P : 2]
+                    nc.tensor.transpose(bank[:, first : first + P], every_2nd, identity[:])
+            grouped = grouped_pool.tile([P, passes * P * PACK], BF16, name="grouped", align_bytes=64)
+            regrouped = bank[:, : 2 * passes * P].rearrange("p (g u r) -> p g r u", u=2, r=P)
+            target = grouped[:].bitcast(F32).rearrange("p (g r u) -> p g r u", u=2, r=P)
+            if len(copied) % VECTOR_COPY_EVERY == VECTOR_COPY_EVERY - 1:
+                nc.vector.tensor_copy(out=target, in_=regrouped)
+            else:
+                nc.scalar.copy(out=target, in_=regrouped)
+            copied.append((grouped, codes, scales))
+            if len(copied) > QUANTISE_LAG:
+                quantise(len(copied) - 1 - QUANTISE_LAG)
+
+        def transpose_unit(parts, codes, scales, unit_banks):
+            part_banks = UNIT_BANKS // len(parts)
+            for b in unit_banks:
+                words = parts[b // part_banks][:].bitcast(F32)
+                first = (b % part_banks) * BANK_WORDS
+                cols = slice(b * PASSES_PER_BANK * P, (b + 1) * PASSES_PER_BANK * P)
+                transpose_bank(
+                    words[:, first : first + BANK_WORDS], PASSES_PER_BANK, codes[:, cols], scales[:, cols]
+                )
+
+        block_order = []
+        for gate in range(GATES):
+            for cell in range(CELLS):
+                for quarter in range(BLOCKS_PER_GATE):
+                    block_order.append((gate, cell, quarter))
+
+        def net_columns(i):
+            gate, cell, quarter = block_order[i]
+            first = ((cell * GATES + gate) * BLOCKS_PER_GATE + quarter) * P
+            return slice(first, first + P)
+
+        wx_blocks = Wx.rearrange("c n (g k) -> (c n) g k", k=K_PASS)
+        x_raw = []
+        for part in range(X_LOADS):
+            x_raw.append(keep.tile([P, IN // X_LOADS], BF16, name="x_raw%d" % part))
+            nc.sync.dma_start(
+                out=x_raw[part][:], in_=input_word[:, part * (IN // X_LOADS) : (part + 1) * (IN // X_LOADS)]
+            )
+        h_raw = keep.tile([P, H], BF16, name="h_raw")
+        nc.sync.dma_start(out=h_raw[:], in_=hidden_states)
+        bias_rows = keep.tile([P, OUT], BF16, name="bias_rows")
+        nc.vector.memset(bias_rows[:].bitcast(I32), 0)
+        nc.sync.dma_start(out=bias_rows[0:1, :], in_=bx.rearrange("(o c) n -> o (c n)", o=1))
+        wh_raw = load_unit(Wh.rearrange("c (b p) k -> p (c b) k", p=P))
+        wx_raw = [load_unit(wx_blocks[net_columns(i), :, :]) for i in range(RAW_UNITS - 1)]
+
+        def load_next_block():
+            if len(wx_raw) < BLOCKS:
+                wx_raw.append(load_unit(wx_blocks[net_columns(len(wx_raw)), :, :]))
+
+        identity = keep.tile([P, P], F32, name="identity")
+        masks.make_identity(nc, identity[:])
+        ones = keep.tile([P, P], BF16, name="ones")
+        nc.vector.memset(ones[:], 1.0)
+        early = keep.tile([P, 1], F32, name="early")
+        nc.vector.memset(early[:], 0.0)
+        nc.scalar.activation(out=early[:], in_=early[:], func=ACT.Sigmoid)
+
+        x_codes = keep.tile([P, X_PASSES * P], U32, name="x_codes", align_bytes=64)
+        x_scales = keep.tile([P, X_PASSES * P], U8, name="x_scales", align_bytes=64)
+        transpose_unit(x_raw, x_codes, x_scales, range(UNIT_BANKS))
+
+        h_codes = keep.tile([P, P], U32, name="h_codes", align_bytes=64)
+        h_scales = keep.tile([P, P], U8, name="h_scales", align_bytes=64)
+        transpose_bank(h_raw[:].bitcast(F32), 1, h_codes[:], h_scales[:])
+
+        bias = keep.tile([P, OUT], F32, name="bias")
+        for j in range(OUT // BANK_WORDS):
+            cols = slice(j * BANK_WORDS, (j + 1) * BANK_WORDS)
+            spread = banks.tile([P, BANK_WORDS], F32, name="bank")
+            nc.tensor.matmul(out=spread[:], lhsT=ones[:], rhs=bias_rows[:, cols], start=True, stop=True)
+            nc.vector.tensor_copy(out=bias[:, cols], in_=spread[:])
+
+        wh_codes = keep.tile([P, BLOCKS * P], U32, name="wh_codes", align_bytes=64)
+        wh_scales = keep.tile([P, BLOCKS * P], U8, name="wh_scales", align_bytes=64)
+        transpose_unit(wh_raw, wh_codes, wh_scales, range(UNIT_BANKS))
+        load_next_block()
+
+        wx_codes = []
+        wx_scales = []
+        net_sums = []
+        nets = []
+        results = keep.tile([P, GATES * CELLS, H], F32, name="results")
+
+        def prepare_first_half(i):
+            wx_codes.append(weight_pool.tile([P, X_PASSES * P], U32, name="codes", align_bytes=64))
+            wx_scales.append(weight_pool.tile([P, X_PASSES * P], U8, name="scales", align_bytes=64))
+            transpose_unit(wx_raw[i], wx_codes[i], wx_scales[i], range(UNIT_BANKS // 2))
+
+        def prepare_second_half(i):
+            transpose_unit(wx_raw[i], wx_codes[i], wx_scales[i], range(UNIT_BANKS // 2, UNIT_BANKS))
+            load_next_block()
+            if i == BLOCKS - 1:
+                for n in range(len(copied) - QUANTISE_LAG, len(copied)):
+                    quantise(n)
+
+        def multiply_first_half(i):
+            net_sums.append(sums.tile([P, P], F32, name="acc"))
+            multiply_input(i, range(X_PASSES // 2))
+
+        def multiply_second_half(i):
+            multiply_input(i, range(X_PASSES // 2, X_PASSES))
+            nc.tensor.matmul_mx(
+                out=net_sums[i][:],
+                lhsT=h_codes[:].bitcast(FP8X4),
+                lhsT_scale=h_scales[:],
+                rhs=wh_codes[:, net_columns(i)].bitcast(FP8X4),
+                rhs_scale=wh_scales[:, net_columns(i)],
+                start=False,
+                stop=True,
+            )
+
+        def multiply_input(i, passes):
+            for g in passes:
+                cols = slice(g * P, (g + 1) * P)
+                nc.tensor.matmul_mx(
+                    out=net_sums[i][:],
+                    lhsT=x_codes[:, cols].bitcast(FP8X4),
+                    lhsT_scale=x_scales[:, cols],
+                    rhs=wx_codes[i][:, cols].bitcast(FP8X4),
+                    rhs_scale=wx_scales[i][:, cols],
+                    start=(g == 0),
+                    stop=False,
+                )
+
+        def add_bias(i):
+            net = out_pool.tile([P, P], F32, name="net")
+            nc.vector.tensor_tensor(out=net[:], in0=net_sums[i][:], in1=bias[:, net_columns(i)], op=ALU.add)
+            nets.append(net)
+
+        def activate(i):
+            gate, cell, quarter = block_order[i]
+            nc.scalar.activation(
+                out=results[:, i // BLOCKS_PER_GATE, quarter * P : (quarter + 1) * P],
+                in_=nets[i][:],
+                func=ACT.Sigmoid if gate == 0 else ACT.Tanh,
+            )
+
+        for i in range(BLOCKS + 3):
+            if i < BLOCKS:
+                prepare_first_half(i)
+            if 0 <= i - 2 < BLOCKS:
+                add_bias(i - 2)
+            if 0 <= i - 3 < BLOCKS:
+                activate(i - 3)
+            if 0 <= i - 1 < BLOCKS:
+                multiply_first_half(i - 1)
+            if i < BLOCKS:
+                prepare_second_half(i)
+            if 0 <= i - 1 < BLOCKS:
+                multiply_second_half(i - 1)
+
+        for i in range(0, BLOCKS, BLOCKS_PER_GATE):
+            gate, cell, quarter = block_order[i]
+            out = out_1 if gate == 0 else out_0
+            nc.sync.dma_start(out=out[:, cell, :], in_=results[:, i // BLOCKS_PER_GATE, :])

@@ -22,22 +22,25 @@ GATES = 2
 OUT = CELLS * GATES * H
 X_PASSES = IN // K_PASS
 BLOCKS = OUT // P
-BLOCKS_PER_GATE = H // P
+
+HALVES = 2
+HALF_PASSES = X_PASSES // HALVES
+HALF_K = HALF_PASSES * K_PASS
+PAIR = 2 * P
+PAIRS = OUT // PAIR
+PAIRS_PER_GATE = H // PAIR
 
 WORDS_PER_PASS = K_PASS // 2
 BANK_WORDS = 512
-PASSES_PER_BANK = BANK_WORDS // WORDS_PER_PASS
-UNIT_BANKS = X_PASSES // PASSES_PER_BANK
-UNIT_LOADS = 2
-LOAD_PASSES = X_PASSES // UNIT_LOADS
-X_LOADS = 4
+RUN = 16
+
+STRIDED = 2
 
 QUANTISE_LAG = 2
-VECTOR_COPY_EVERY = 4
+VECTOR_COPY_EVERY = 16
 
-RAW_UNITS = 6
-TRANSPOSE_BANKS = 6
-SUM_BANKS = 2
+RAW_TILES = 12
+TRANSPOSE_BANKS = 7
 
 FLOPS = 2 * P * OUT * (IN + H)
 
@@ -46,88 +49,69 @@ def tile_compute_gate_k_kernel(tc, input_word, hidden_states, Wx, bx, Wh, out_0,
     nc = tc.nc
     with ExitStack() as ctx:
         keep = ctx.enter_context(tc.tile_pool(name="keep", bufs=1))
-        raw_pool = ctx.enter_context(tc.tile_pool(name="raw", bufs=RAW_UNITS * UNIT_LOADS))
+        raw_pool = ctx.enter_context(tc.tile_pool(name="raw", bufs=RAW_TILES))
+        permuted_pool = ctx.enter_context(tc.tile_pool(name="permuted", bufs=4))
         grouped_pool = ctx.enter_context(tc.tile_pool(name="grouped", bufs=QUANTISE_LAG + 4))
-        weight_pool = ctx.enter_context(tc.tile_pool(name="weight", bufs=3))
-        out_pool = ctx.enter_context(tc.tile_pool(name="out", bufs=3))
+        weight_pool = ctx.enter_context(tc.tile_pool(name="weight", bufs=2))
+        out_pool = ctx.enter_context(tc.tile_pool(name="out", bufs=2))
         banks = ctx.enter_context(tc.psum_pool(name="banks", bufs=TRANSPOSE_BANKS))
-        sums = ctx.enter_context(tc.psum_pool(name="sums", bufs=SUM_BANKS))
+        sums = ctx.enter_context(tc.psum_pool(name="sums", bufs=1))
         ctx.enter_context(tc.manual_schedule())
 
-        def load_unit(rows):
-            parts = []
-            for part in range(UNIT_LOADS):
-                raw = raw_pool.tile([P, LOAD_PASSES * K_PASS], BF16, name="raw")
-                nc.sync.dma_start(
-                    out=raw[:].rearrange("p (g k) -> p g k", k=K_PASS),
-                    in_=rows[:, part * LOAD_PASSES : (part + 1) * LOAD_PASSES, :],
-                )
-                parts.append(raw)
-            return parts
-
-        copied = []
-
-        def quantise(n):
-            grouped, codes, scales = copied[n]
-            nc.vector.quantize_mx(out=codes.bitcast(FP8X4), scales=scales, in_=grouped[:])
-
-        def transpose_bank(words, passes, codes, scales):
-            bank = banks.tile([P, BANK_WORDS], F32, name="bank")
-            for g in range(passes):
-                for u in range(2):
-                    first = (2 * g + u) * P
-                    every_2nd = words[:, 2 * g * P + u : 2 * (g + 1) * P : 2]
-                    nc.tensor.transpose(bank[:, first : first + P], every_2nd, identity[:])
-            grouped = grouped_pool.tile([P, passes * P * PACK], BF16, name="grouped", align_bytes=64)
-            regrouped = bank[:, : 2 * passes * P].rearrange("p (g u r) -> p g r u", u=2, r=P)
-            target = grouped[:].bitcast(F32).rearrange("p (g r u) -> p g r u", u=2, r=P)
-            if len(copied) % VECTOR_COPY_EVERY == VECTOR_COPY_EVERY - 1:
-                nc.vector.tensor_copy(out=target, in_=regrouped)
-            else:
-                nc.scalar.copy(out=target, in_=regrouped)
-            copied.append((grouped, codes, scales))
-            if len(copied) > QUANTISE_LAG:
-                quantise(len(copied) - 1 - QUANTISE_LAG)
-
-        def transpose_unit(parts, codes, scales, unit_banks):
-            part_banks = UNIT_BANKS // len(parts)
-            for b in unit_banks:
-                words = parts[b // part_banks][:].bitcast(F32)
-                first = (b % part_banks) * BANK_WORDS
-                cols = slice(b * PASSES_PER_BANK * P, (b + 1) * PASSES_PER_BANK * P)
-                transpose_bank(
-                    words[:, first : first + BANK_WORDS], PASSES_PER_BANK, codes[:, cols], scales[:, cols]
-                )
-
-        block_order = []
+        pair_order = []
         for gate in range(GATES):
             for cell in range(CELLS):
-                for quarter in range(BLOCKS_PER_GATE):
-                    block_order.append((gate, cell, quarter))
+                for part in range(PAIRS_PER_GATE):
+                    pair_order.append((gate, cell, part))
 
         def net_columns(i):
-            gate, cell, quarter = block_order[i]
-            first = ((cell * GATES + gate) * BLOCKS_PER_GATE + quarter) * P
-            return slice(first, first + P)
+            gate, cell, part = pair_order[i]
+            first = (cell * GATES + gate) * H + part * PAIR
+            return slice(first, first + PAIR)
 
-        wx_blocks = Wx.rearrange("c n (g k) -> (c n) g k", k=K_PASS)
+        wx_rows = Wx.rearrange("c n k -> (c n) k")
+        wx_raw = []
+
+        def load_next_half_pair():
+            if len(wx_raw) < PAIRS * HALVES:
+                i, half = divmod(len(wx_raw), HALVES)
+                first = net_columns(i).start
+                tiles = []
+                for block in range(PAIR // P):
+                    raw = raw_pool.tile([P, HALF_K], BF16, name="raw")
+                    nc.sync.dma_start(
+                        out=raw[:],
+                        in_=wx_rows[first + block * P : first + (block + 1) * P, half * HALF_K : (half + 1) * HALF_K],
+                    )
+                    tiles.append(raw)
+                wx_raw.append(tiles)
+
         x_raw = []
-        for part in range(X_LOADS):
-            x_raw.append(keep.tile([P, IN // X_LOADS], BF16, name="x_raw%d" % part))
-            nc.sync.dma_start(
-                out=x_raw[part][:], in_=input_word[:, part * (IN // X_LOADS) : (part + 1) * (IN // X_LOADS)]
-            )
+        for half in range(HALVES):
+            raw = raw_pool.tile([P, HALF_K], BF16, name="raw")
+            for part in range(2):
+                cols = slice(part * HALF_K // 2, (part + 1) * HALF_K // 2)
+                nc.sync.dma_start(
+                    out=raw[:, cols],
+                    in_=input_word[:, half * HALF_K + cols.start : half * HALF_K + cols.stop],
+                )
+            x_raw.append(raw)
         h_raw = keep.tile([P, H], BF16, name="h_raw")
         nc.sync.dma_start(out=h_raw[:], in_=hidden_states)
         bias_rows = keep.tile([P, OUT], BF16, name="bias_rows")
         nc.vector.memset(bias_rows[:].bitcast(I32), 0)
         nc.sync.dma_start(out=bias_rows[0:1, :], in_=bx.rearrange("(o c) n -> o (c n)", o=1))
-        wh_raw = load_unit(Wh.rearrange("c (b p) k -> p (c b) k", p=P))
-        wx_raw = [load_unit(wx_blocks[net_columns(i), :, :]) for i in range(RAW_UNITS - 1)]
-
-        def load_next_block():
-            if len(wx_raw) < BLOCKS:
-                wx_raw.append(load_unit(wx_blocks[net_columns(len(wx_raw)), :, :]))
+        wh_blocks = Wh.rearrange("c (b p) k -> p (c b) k", p=P)
+        wh_raw = []
+        for half in range(HALVES):
+            raw = raw_pool.tile([P, HALF_K], BF16, name="raw")
+            nc.sync.dma_start(
+                out=raw[:].rearrange("p (b k) -> p b k", k=K_PASS),
+                in_=wh_blocks[:, half * HALF_PASSES : (half + 1) * HALF_PASSES, :],
+            )
+            wh_raw.append(raw)
+        for n in range((RAW_TILES - 2 * HALVES) // 2):
+            load_next_half_pair()
 
         identity = keep.tile([P, P], F32, name="identity")
         masks.make_identity(nc, identity[:])
@@ -139,99 +123,157 @@ def tile_compute_gate_k_kernel(tc, input_word, hidden_states, Wx, bx, Wh, out_0,
 
         x_codes = keep.tile([P, X_PASSES * P], U32, name="x_codes", align_bytes=64)
         x_scales = keep.tile([P, X_PASSES * P], U8, name="x_scales", align_bytes=64)
-        transpose_unit(x_raw, x_codes, x_scales, range(UNIT_BANKS))
-
         h_codes = keep.tile([P, P], U32, name="h_codes", align_bytes=64)
         h_scales = keep.tile([P, P], U8, name="h_scales", align_bytes=64)
-        transpose_bank(h_raw[:].bitcast(F32), 1, h_codes[:], h_scales[:])
-
+        wh_codes = keep.tile([P, OUT], U32, name="wh_codes", align_bytes=64)
+        wh_scales = keep.tile([P, OUT], U8, name="wh_scales", align_bytes=64)
+        wx_codes = []
+        wx_scales = []
         bias = keep.tile([P, OUT], F32, name="bias")
+        results = keep.tile([P, GATES * CELLS, H], F32, name="results")
+        net_sums = []
+        nets = []
+
+        def permute(raw):
+            permuted = permuted_pool.tile([P, (HALF_PASSES - STRIDED) * K_PASS], BF16, name="permuted")
+            nc.vector.tensor_copy(
+                out=permuted[:].rearrange("p (u b i) -> p u b i", u=2, i=RUN),
+                in_=raw[:, STRIDED * K_PASS :].rearrange("p (b u i) -> p u b i", u=2, i=RUN),
+            )
+            return permuted
+
+        def windows(raw, permuted, g):
+            if permuted is None or g < STRIDED:
+                words = raw[:].bitcast(F32)
+                first = g * WORDS_PER_PASS
+                return [words[:, first + u : first + WORDS_PER_PASS : 2] for u in range(2)]
+            words = permuted[:].bitcast(F32)
+            second_half = (HALF_PASSES - STRIDED) * P
+            first = (g - STRIDED) * P
+            return [words[:, u * second_half + first : u * second_half + first + P] for u in range(2)]
+
+        copied = []
+
+        def quantise(n):
+            grouped, codes, scales = copied[n]
+            nc.vector.quantize_mx(out=codes.bitcast(FP8X4), scales=scales, in_=grouped[:])
+
+        def transpose_bank(stationaries, codes, scales):
+            bank = banks.tile([P, BANK_WORDS], F32, name="bank")
+            for i, stationary in enumerate(stationaries):
+                nc.tensor.transpose(bank[:, i * P : (i + 1) * P], stationary, identity[:])
+            width = len(stationaries) * P
+            grouped = grouped_pool.tile([P, 2 * width], BF16, name="grouped", align_bytes=64)
+            regrouped = bank[:, :width].rearrange("p (g u r) -> p g r u", u=2, r=P)
+            target = grouped[:].bitcast(F32).rearrange("p (g r u) -> p g r u", u=2, r=P)
+            if len(copied) % VECTOR_COPY_EVERY == VECTOR_COPY_EVERY - 1:
+                nc.vector.tensor_copy(out=target, in_=regrouped)
+            else:
+                nc.scalar.copy(out=target, in_=regrouped)
+            copied.append((grouped, codes, scales))
+            if len(copied) > QUANTISE_LAG:
+                quantise(len(copied) - 1 - QUANTISE_LAG)
+
+        def one_operand_banks(raw, permuted, codes, scales, first_pass):
+            for b in range(HALF_PASSES // 2):
+                cols = slice((first_pass + 2 * b) * P, (first_pass + 2 * b + 2) * P)
+                stationaries = windows(raw, permuted, 2 * b) + windows(raw, permuted, 2 * b + 1)
+                transpose_bank(stationaries, codes[:, cols], scales[:, cols])
+
+        x_permuted = [permute(x_raw[0])]
+        one_operand_banks(x_raw[0], x_permuted[0], x_codes, x_scales, 0)
+        x_permuted.append(permute(x_raw[1]))
+        one_operand_banks(x_raw[1], x_permuted[1], x_codes, x_scales, HALF_PASSES)
+        transpose_bank(windows(h_raw, None, 0), h_codes[:], h_scales[:])
+
         for j in range(OUT // BANK_WORDS):
             cols = slice(j * BANK_WORDS, (j + 1) * BANK_WORDS)
             spread = banks.tile([P, BANK_WORDS], F32, name="bank")
             nc.tensor.matmul(out=spread[:], lhsT=ones[:], rhs=bias_rows[:, cols], start=True, stop=True)
             nc.vector.tensor_copy(out=bias[:, cols], in_=spread[:])
 
-        wh_codes = keep.tile([P, BLOCKS * P], U32, name="wh_codes", align_bytes=64)
-        wh_scales = keep.tile([P, BLOCKS * P], U8, name="wh_scales", align_bytes=64)
-        transpose_unit(wh_raw, wh_codes, wh_scales, range(UNIT_BANKS))
-        load_next_block()
+        one_operand_banks(wh_raw[0], None, wh_codes, wh_scales, 0)
+        load_next_half_pair()
+        one_operand_banks(wh_raw[1], None, wh_codes, wh_scales, HALF_PASSES)
+        load_next_half_pair()
 
-        wx_codes = []
-        wx_scales = []
-        net_sums = []
-        nets = []
-        results = keep.tile([P, GATES * CELLS, H], F32, name="results")
-
-        def prepare_first_half(i):
-            wx_codes.append(weight_pool.tile([P, X_PASSES * P], U32, name="codes", align_bytes=64))
-            wx_scales.append(weight_pool.tile([P, X_PASSES * P], U8, name="scales", align_bytes=64))
-            transpose_unit(wx_raw[i], wx_codes[i], wx_scales[i], range(UNIT_BANKS // 2))
-
-        def prepare_second_half(i):
-            transpose_unit(wx_raw[i], wx_codes[i], wx_scales[i], range(UNIT_BANKS // 2, UNIT_BANKS))
-            load_next_block()
-            if i == BLOCKS - 1:
-                for n in range(len(copied) - QUANTISE_LAG, len(copied)):
-                    quantise(n)
-
-        def multiply_first_half(i):
-            net_sums.append(sums.tile([P, P], F32, name="acc"))
-            multiply_input(i, range(X_PASSES // 2))
-
-        def multiply_second_half(i):
-            multiply_input(i, range(X_PASSES // 2, X_PASSES))
-            nc.tensor.matmul_mx(
-                out=net_sums[i][:],
-                lhsT=h_codes[:].bitcast(FP8X4),
-                lhsT_scale=h_scales[:],
-                rhs=wh_codes[:, net_columns(i)].bitcast(FP8X4),
-                rhs_scale=wh_scales[:, net_columns(i)],
-                start=False,
-                stop=True,
-            )
-
-        def multiply_input(i, passes):
-            for g in passes:
-                cols = slice(g * P, (g + 1) * P)
+        def multiply(n):
+            i, half = divmod(n, HALVES)
+            if half == 0:
+                net_sums.append(sums.tile([P, BANK_WORDS], F32, name="acc"))
+            acc = net_sums[i][:, :PAIR]
+            for g in range(half * HALF_PASSES, (half + 1) * HALF_PASSES):
+                x_cols = slice(g * P, (g + 1) * P)
+                w_cols = slice(g * PAIR, (g + 1) * PAIR)
                 nc.tensor.matmul_mx(
-                    out=net_sums[i][:],
-                    lhsT=x_codes[:, cols].bitcast(FP8X4),
-                    lhsT_scale=x_scales[:, cols],
-                    rhs=wx_codes[i][:, cols].bitcast(FP8X4),
-                    rhs_scale=wx_scales[i][:, cols],
+                    out=acc,
+                    lhsT=x_codes[:, x_cols].bitcast(FP8X4),
+                    lhsT_scale=x_scales[:, x_cols],
+                    rhs=wx_codes[i][:, w_cols].bitcast(FP8X4),
+                    rhs_scale=wx_scales[i][:, w_cols],
                     start=(g == 0),
                     stop=False,
                 )
+            if half == HALVES - 1:
+                nc.tensor.matmul_mx(
+                    out=acc,
+                    lhsT=h_codes[:].bitcast(FP8X4),
+                    lhsT_scale=h_scales[:],
+                    rhs=wh_codes[:, net_columns(i)].bitcast(FP8X4),
+                    rhs_scale=wh_scales[:, net_columns(i)],
+                    start=False,
+                    stop=True,
+                )
 
-        def add_bias(i):
-            net = out_pool.tile([P, P], F32, name="net")
-            nc.vector.tensor_tensor(out=net[:], in0=net_sums[i][:], in1=bias[:, net_columns(i)], op=ALU.add)
-            nets.append(net)
+        def add_bias(n):
+            i, half = divmod(n, HALVES)
+            if half == HALVES - 1:
+                net = out_pool.tile([P, PAIR], F32, name="net")
+                nc.vector.tensor_tensor(out=net[:], in0=net_sums[i][:, :PAIR], in1=bias[:, net_columns(i)], op=ALU.add)
+                nets.append(net)
 
-        def activate(i):
-            gate, cell, quarter = block_order[i]
-            nc.scalar.activation(
-                out=results[:, i // BLOCKS_PER_GATE, quarter * P : (quarter + 1) * P],
-                in_=nets[i][:],
-                func=ACT.Sigmoid if gate == 0 else ACT.Tanh,
-            )
+        def activate(n):
+            i, half = divmod(n, HALVES)
+            if half == HALVES - 1:
+                gate, cell, part = pair_order[i]
+                nc.scalar.activation(
+                    out=results[:, i // PAIRS_PER_GATE, part * PAIR : (part + 1) * PAIR],
+                    in_=nets[i][:],
+                    func=ACT.Sigmoid if gate == 0 else ACT.Tanh,
+                )
 
-        for i in range(BLOCKS + 3):
-            if i < BLOCKS:
-                prepare_first_half(i)
-            if 0 <= i - 2 < BLOCKS:
-                add_bias(i - 2)
-            if 0 <= i - 3 < BLOCKS:
-                activate(i - 3)
-            if 0 <= i - 1 < BLOCKS:
-                multiply_first_half(i - 1)
-            if i < BLOCKS:
-                prepare_second_half(i)
-            if 0 <= i - 1 < BLOCKS:
-                multiply_second_half(i - 1)
+        wx_permuted = [[permute(raw) for raw in wx_raw[0]]]
+        for n in range(PAIRS * HALVES):
+            i, half = divmod(n, HALVES)
+            if half == 0:
+                wx_codes.append(weight_pool.tile([P, X_PASSES * PAIR], U32, name="codes", align_bytes=64))
+                wx_scales.append(weight_pool.tile([P, X_PASSES * PAIR], U8, name="scales", align_bytes=64))
+            for g in range(HALF_PASSES):
+                stationaries = []
+                for block in range(PAIR // P):
+                    stationaries += windows(wx_raw[n][block], wx_permuted[n][block], g)
+                cols = slice((half * HALF_PASSES + g) * PAIR, (half * HALF_PASSES + g + 1) * PAIR)
+                transpose_bank(stationaries, wx_codes[i][:, cols], wx_scales[i][:, cols])
+                if g == 3 and n > 0:
+                    multiply(n - 1)
+                if g == 4 and n + 1 < len(wx_raw):
+                    wx_permuted.append([permute(wx_raw[n + 1][0])])
+                if g == 5 and n > 0:
+                    add_bias(n - 1)
+                if g == 6 and n + 1 < len(wx_raw):
+                    wx_permuted[n + 1].append(permute(wx_raw[n + 1][1]))
+                if g == 7 and n > 0:
+                    activate(n - 1)
+            load_next_half_pair()
 
-        for i in range(0, BLOCKS, BLOCKS_PER_GATE):
-            gate, cell, quarter = block_order[i]
+        last = PAIRS * HALVES - 1
+        for n in range(len(copied) - QUANTISE_LAG, len(copied)):
+            quantise(n)
+        multiply(last)
+        add_bias(last)
+        activate(last)
+
+        for j in range(GATES * CELLS):
+            gate, cell, part = pair_order[j * PAIRS_PER_GATE]
             out = out_1 if gate == 0 else out_0
-            nc.sync.dma_start(out=out[:, cell, :], in_=results[:, i // BLOCKS_PER_GATE, :])
+            nc.sync.dma_start(out=out[:, cell, :], in_=results[:, j, :])

@@ -26,6 +26,7 @@ BLOCKS = OUT // P
 HALVES = 2
 HALF_PASSES = X_PASSES // HALVES
 HALF_K = HALF_PASSES * K_PASS
+BURST = 4
 PAIR = 2 * P
 PAIRS = OUT // PAIR
 PAIRS_PER_GATE = H // PAIR
@@ -34,13 +35,12 @@ WORDS_PER_PASS = K_PASS // 2
 BANK_WORDS = 512
 RUN = 16
 
-STRIDED = 2
-
 QUANTISE_LAG = 2
-VECTOR_COPY_EVERY = 16
+VECTOR_COPY_EVERY = 24
 
 RAW_TILES = 12
-TRANSPOSE_BANKS = 7
+TRANSPOSE_BANKS = 6
+SUM_BANKS = 2
 
 FLOPS = 2 * P * OUT * (IN + H)
 
@@ -55,7 +55,7 @@ def tile_compute_gate_k_kernel(tc, input_word, hidden_states, Wx, bx, Wh, out_0,
         weight_pool = ctx.enter_context(tc.tile_pool(name="weight", bufs=2))
         out_pool = ctx.enter_context(tc.tile_pool(name="out", bufs=2))
         banks = ctx.enter_context(tc.psum_pool(name="banks", bufs=TRANSPOSE_BANKS))
-        sums = ctx.enter_context(tc.psum_pool(name="sums", bufs=1))
+        sums = ctx.enter_context(tc.psum_pool(name="sums", bufs=SUM_BANKS))
         ctx.enter_context(tc.manual_schedule())
 
         pair_order = []
@@ -135,22 +135,23 @@ def tile_compute_gate_k_kernel(tc, input_word, hidden_states, Wx, bx, Wh, out_0,
         nets = []
 
         def permute(raw):
-            permuted = permuted_pool.tile([P, (HALF_PASSES - STRIDED) * K_PASS], BF16, name="permuted")
+            firsts = permuted_pool.tile([P, HALF_K // 2], BF16, name="firsts")
+            runs = raw[:].rearrange("p (s n u i) -> p s n u i", s=2, u=2, i=RUN)
             nc.vector.tensor_copy(
-                out=permuted[:].rearrange("p (u b i) -> p u b i", u=2, i=RUN),
-                in_=raw[:, STRIDED * K_PASS :].rearrange("p (b u i) -> p u b i", u=2, i=RUN),
+                out=firsts[:].rearrange("p (n s i) -> p n s i", s=2, i=RUN),
+                in_=raw[:].rearrange("p (s n u i) -> p u n s i", s=2, u=2, i=RUN)[:, 0],
             )
-            return permuted
+            nc.vector.tensor_copy(out=runs[:, 1, :, 0, :], in_=runs[:, 0, :, 1, :])
+            return firsts
 
         def windows(raw, permuted, g):
-            if permuted is None or g < STRIDED:
-                words = raw[:].bitcast(F32)
+            words = raw[:].bitcast(F32)
+            if permuted is None:
                 first = g * WORDS_PER_PASS
                 return [words[:, first + u : first + WORDS_PER_PASS : 2] for u in range(2)]
-            words = permuted[:].bitcast(F32)
-            second_half = (HALF_PASSES - STRIDED) * P
-            first = (g - STRIDED) * P
-            return [words[:, u * second_half + first : u * second_half + first + P] for u in range(2)]
+            first = g * P
+            seconds = HALF_K // 4 + first
+            return [permuted[:].bitcast(F32)[:, first : first + P], words[:, seconds : seconds + P]]
 
         copied = []
 
@@ -197,12 +198,13 @@ def tile_compute_gate_k_kernel(tc, input_word, hidden_states, Wx, bx, Wh, out_0,
         one_operand_banks(wh_raw[1], None, wh_codes, wh_scales, HALF_PASSES)
         load_next_half_pair()
 
-        def multiply(n):
+        def multiply(n, burst):
             i, half = divmod(n, HALVES)
-            if half == 0:
+            if half == 0 and burst == 0:
                 net_sums.append(sums.tile([P, BANK_WORDS], F32, name="acc"))
             acc = net_sums[i][:, :PAIR]
-            for g in range(half * HALF_PASSES, (half + 1) * HALF_PASSES):
+            first = half * HALF_PASSES + burst * BURST
+            for g in range(first, first + BURST):
                 x_cols = slice(g * P, (g + 1) * P)
                 w_cols = slice(g * PAIR, (g + 1) * PAIR)
                 nc.tensor.matmul_mx(
@@ -214,7 +216,7 @@ def tile_compute_gate_k_kernel(tc, input_word, hidden_states, Wx, bx, Wh, out_0,
                     start=(g == 0),
                     stop=False,
                 )
-            if half == HALVES - 1:
+            if first + BURST == X_PASSES:
                 nc.tensor.matmul_mx(
                     out=acc,
                     lhsT=h_codes[:].bitcast(FP8X4),
@@ -254,22 +256,25 @@ def tile_compute_gate_k_kernel(tc, input_word, hidden_states, Wx, bx, Wh, out_0,
                     stationaries += windows(wx_raw[n][block], wx_permuted[n][block], g)
                 cols = slice((half * HALF_PASSES + g) * PAIR, (half * HALF_PASSES + g + 1) * PAIR)
                 transpose_bank(stationaries, wx_codes[i][:, cols], wx_scales[i][:, cols])
+                if g == 1 and n > 1:
+                    add_bias(n - 2)
+                if g == 3 and n > 1:
+                    activate(n - 2)
                 if g == 3 and n > 0:
-                    multiply(n - 1)
-                if g == 4 and n + 1 < len(wx_raw):
+                    multiply(n - 1, 0)
+                if g == 0 and n + 1 < len(wx_raw):
                     wx_permuted.append([permute(wx_raw[n + 1][0])])
-                if g == 5 and n > 0:
-                    add_bias(n - 1)
-                if g == 6 and n + 1 < len(wx_raw):
+                if g == 3 and n + 1 < len(wx_raw):
                     wx_permuted[n + 1].append(permute(wx_raw[n + 1][1]))
                 if g == 7 and n > 0:
-                    activate(n - 1)
+                    multiply(n - 1, 1)
             load_next_half_pair()
 
         last = PAIRS * HALVES - 1
         for n in range(len(copied) - QUANTISE_LAG, len(copied)):
             quantise(n)
-        multiply(last)
+        multiply(last, 0)
+        multiply(last, 1)
         add_bias(last)
         activate(last)
 

@@ -34,11 +34,14 @@ PAIRS_PER_GATE = H // PAIR
 WORDS_PER_PASS = K_PASS // 2
 BANK_WORDS = 512
 RUN = 16
+STRIDED = 2
+MOVED = HALF_PASSES - STRIDED
+BLOCKS_PER_PAIR = PAIR // P
+QUANTISE_BANKS = 2
 
-QUANTISE_LAG = 2
-VECTOR_COPY_EVERY = 24
+VECTOR_COPY_EVERY = 16
 
-RAW_TILES = 12
+RAW_TILES = 6
 TRANSPOSE_BANKS = 6
 SUM_BANKS = 2
 
@@ -50,8 +53,8 @@ def tile_compute_gate_k_kernel(tc, input_word, hidden_states, Wx, bx, Wh, out_0,
     with ExitStack() as ctx:
         keep = ctx.enter_context(tc.tile_pool(name="keep", bufs=1))
         raw_pool = ctx.enter_context(tc.tile_pool(name="raw", bufs=RAW_TILES))
-        permuted_pool = ctx.enter_context(tc.tile_pool(name="permuted", bufs=4))
-        grouped_pool = ctx.enter_context(tc.tile_pool(name="grouped", bufs=QUANTISE_LAG + 4))
+        firsts_pool = ctx.enter_context(tc.tile_pool(name="firsts", bufs=2))
+        grouped_pool = ctx.enter_context(tc.tile_pool(name="grouped", bufs=4))
         weight_pool = ctx.enter_context(tc.tile_pool(name="weight", bufs=2))
         out_pool = ctx.enter_context(tc.tile_pool(name="out", bufs=2))
         banks = ctx.enter_context(tc.psum_pool(name="banks", bufs=TRANSPOSE_BANKS))
@@ -76,41 +79,31 @@ def tile_compute_gate_k_kernel(tc, input_word, hidden_states, Wx, bx, Wh, out_0,
             if len(wx_raw) < PAIRS * HALVES:
                 i, half = divmod(len(wx_raw), HALVES)
                 first = net_columns(i).start
-                tiles = []
-                for block in range(PAIR // P):
-                    raw = raw_pool.tile([P, HALF_K], BF16, name="raw")
-                    nc.sync.dma_start(
-                        out=raw[:],
-                        in_=wx_rows[first + block * P : first + (block + 1) * P, half * HALF_K : (half + 1) * HALF_K],
-                    )
-                    tiles.append(raw)
-                wx_raw.append(tiles)
+                raw = raw_pool.tile([P, BLOCKS_PER_PAIR, HALF_K], BF16, name="raw")
+                for block in range(BLOCKS_PER_PAIR):
+                    rows = slice(first + block * P, first + (block + 1) * P)
+                    nc.sync.dma_start(out=raw[:, block, :], in_=wx_rows[rows, half * HALF_K : (half + 1) * HALF_K])
+                wx_raw.append(raw)
 
-        x_raw = []
+        x_raw = raw_pool.tile([P, HALVES, HALF_K], BF16, name="raw")
         for half in range(HALVES):
-            raw = raw_pool.tile([P, HALF_K], BF16, name="raw")
             for part in range(2):
                 cols = slice(part * HALF_K // 2, (part + 1) * HALF_K // 2)
+                first = half * HALF_K
                 nc.sync.dma_start(
-                    out=raw[:, cols],
-                    in_=input_word[:, half * HALF_K + cols.start : half * HALF_K + cols.stop],
+                    out=x_raw[:, half, cols], in_=input_word[:, first + cols.start : first + cols.stop]
                 )
-            x_raw.append(raw)
-        h_raw = keep.tile([P, H], BF16, name="h_raw")
-        nc.sync.dma_start(out=h_raw[:], in_=hidden_states)
+        h_raw = keep.tile([P, 1, H], BF16, name="h_raw")
+        nc.sync.dma_start(out=h_raw[:, 0, :], in_=hidden_states)
         bias_rows = keep.tile([P, OUT], BF16, name="bias_rows")
         nc.vector.memset(bias_rows[:].bitcast(I32), 0)
         nc.sync.dma_start(out=bias_rows[0:1, :], in_=bx.rearrange("(o c) n -> o (c n)", o=1))
         wh_blocks = Wh.rearrange("c (b p) k -> p (c b) k", p=P)
-        wh_raw = []
-        for half in range(HALVES):
-            raw = raw_pool.tile([P, HALF_K], BF16, name="raw")
-            nc.sync.dma_start(
-                out=raw[:].rearrange("p (b k) -> p b k", k=K_PASS),
-                in_=wh_blocks[:, half * HALF_PASSES : (half + 1) * HALF_PASSES, :],
-            )
-            wh_raw.append(raw)
-        for n in range((RAW_TILES - 2 * HALVES) // 2):
+        wh_raw = raw_pool.tile([P, BLOCKS, K_PASS], BF16, name="raw")
+        for half in range(2):
+            some = slice(half * BLOCKS // 2, (half + 1) * BLOCKS // 2)
+            nc.sync.dma_start(out=wh_raw[:, some, :], in_=wh_blocks[:, some, :])
+        for n in range(RAW_TILES - 2):
             load_next_half_pair()
 
         identity = keep.tile([P, P], F32, name="identity")
@@ -134,58 +127,80 @@ def tile_compute_gate_k_kernel(tc, input_word, hidden_states, Wx, bx, Wh, out_0,
         net_sums = []
         nets = []
 
-        def permute(raw):
-            firsts = permuted_pool.tile([P, HALF_K // 2], BF16, name="firsts")
-            runs = raw[:].rearrange("p (s n u i) -> p s n u i", s=2, u=2, i=RUN)
-            nc.vector.tensor_copy(
-                out=firsts[:].rearrange("p (n s i) -> p n s i", s=2, i=RUN),
-                in_=raw[:].rearrange("p (s n u i) -> p u n s i", s=2, u=2, i=RUN)[:, 0],
-            )
-            nc.vector.tensor_copy(out=runs[:, 1, :, 0, :], in_=runs[:, 0, :, 1, :])
-            return firsts
+        def new_firsts():
+            return firsts_pool.tile([P, 2, MOVED * P * 2], BF16, name="firsts")
 
-        def windows(raw, permuted, g):
-            words = raw[:].bitcast(F32)
-            if permuted is None:
+        def gather_firsts(raw, firsts, blocks):
+            nc.vector.tensor_copy(
+                out=firsts[:, blocks, :].rearrange("p k (n s i) -> p k n s i", s=2, i=RUN),
+                in_=raw[:, blocks, STRIDED * K_PASS :].rearrange("p k (s n u i) -> p u k n s i", s=2, u=2, i=RUN)[:, 0],
+            )
+
+        def move_seconds(raw, blocks):
+            runs = raw[:, blocks, STRIDED * K_PASS :].rearrange("p k (s n u i) -> p s u k n i", s=2, u=2, i=RUN)
+            nc.vector.tensor_copy(out=runs[:, 1, 0], in_=runs[:, 0, 1])
+
+        def windows(raw, firsts, block, g):
+            words = raw[:, block, :].bitcast(F32)
+            if firsts is None or g < STRIDED:
                 first = g * WORDS_PER_PASS
                 return [words[:, first + u : first + WORDS_PER_PASS : 2] for u in range(2)]
-            first = g * P
-            seconds = HALF_K // 4 + first
-            return [permuted[:].bitcast(F32)[:, first : first + P], words[:, seconds : seconds + P]]
+            first = (g - STRIDED) * P
+            second = STRIDED * WORDS_PER_PASS + MOVED * P + first
+            return [firsts[:, block, :].bitcast(F32)[:, first : first + P], words[:, second : second + P]]
 
         copied = []
+        counts = {"banks": 0}
 
-        def quantise(n):
-            grouped, codes, scales = copied[n]
-            nc.vector.quantize_mx(out=codes.bitcast(FP8X4), scales=scales, in_=grouped[:])
+        def quantise(grouped, codes, scales):
+            nc.vector.quantize_mx(out=codes.bitcast(FP8X4), scales=scales, in_=grouped)
 
-        def transpose_bank(stationaries, codes, scales):
+        def transpose_bank(stationaries, grouped):
             bank = banks.tile([P, BANK_WORDS], F32, name="bank")
             for i, stationary in enumerate(stationaries):
                 nc.tensor.transpose(bank[:, i * P : (i + 1) * P], stationary, identity[:])
             width = len(stationaries) * P
-            grouped = grouped_pool.tile([P, 2 * width], BF16, name="grouped", align_bytes=64)
             regrouped = bank[:, :width].rearrange("p (g u r) -> p g r u", u=2, r=P)
-            target = grouped[:].bitcast(F32).rearrange("p (g r u) -> p g r u", u=2, r=P)
-            if len(copied) % VECTOR_COPY_EVERY == VECTOR_COPY_EVERY - 1:
+            target = grouped.bitcast(F32).rearrange("p (g r u) -> p g r u", u=2, r=P)
+            if counts["banks"] % VECTOR_COPY_EVERY == VECTOR_COPY_EVERY - 1:
                 nc.vector.tensor_copy(out=target, in_=regrouped)
             else:
                 nc.scalar.copy(out=target, in_=regrouped)
-            copied.append((grouped, codes, scales))
-            if len(copied) > QUANTISE_LAG:
-                quantise(len(copied) - 1 - QUANTISE_LAG)
+            counts["banks"] += 1
 
-        def one_operand_banks(raw, permuted, codes, scales, first_pass):
-            for b in range(HALF_PASSES // 2):
-                cols = slice((first_pass + 2 * b) * P, (first_pass + 2 * b + 2) * P)
-                stationaries = windows(raw, permuted, 2 * b) + windows(raw, permuted, 2 * b + 1)
-                transpose_bank(stationaries, codes[:, cols], scales[:, cols])
+        def prepare(jobs, codes, scales, after_bank):
+            for b, stationaries in enumerate(jobs):
+                width = BANK_WORDS * 2
+                if b % QUANTISE_BANKS == 0:
+                    grouped = grouped_pool.tile([P, QUANTISE_BANKS * width], BF16, name="grouped", align_bytes=64)
+                part = b % QUANTISE_BANKS
+                transpose_bank(stationaries, grouped[:, part * width : (part + 1) * width])
+                if part == QUANTISE_BANKS - 1:
+                    cols = slice((b - part) * PAIR, (b + 1) * PAIR)
+                    copied.append((grouped[:], codes[:, cols], scales[:, cols]))
+                    if len(copied) > 1:
+                        quantise(*copied.pop(0))
+                after_bank(b)
 
-        x_permuted = [permute(x_raw[0])]
-        one_operand_banks(x_raw[0], x_permuted[0], x_codes, x_scales, 0)
-        x_permuted.append(permute(x_raw[1]))
-        one_operand_banks(x_raw[1], x_permuted[1], x_codes, x_scales, HALF_PASSES)
-        transpose_bank(windows(h_raw, None, 0), h_codes[:], h_scales[:])
+        x_firsts = new_firsts()
+
+        def move_x(half):
+            gather_firsts(x_raw, x_firsts, slice(half, half + 1))
+            move_seconds(x_raw, slice(half, half + 1))
+
+        def after_x_bank(b):
+            if b == 2:
+                move_x(1)
+
+        x_jobs = []
+        for g in range(0, X_PASSES, 2):
+            half, first = divmod(g, HALF_PASSES)
+            x_jobs.append(windows(x_raw, x_firsts, half, first) + windows(x_raw, x_firsts, half, first + 1))
+        move_x(0)
+        prepare(x_jobs, x_codes, x_scales, after_x_bank)
+        h_grouped = keep.tile([P, H], BF16, name="h_grouped", align_bytes=64)
+        transpose_bank(windows(h_raw, None, 0, 0), h_grouped[:])
+        quantise(*copied.pop(0))
 
         for j in range(OUT // BANK_WORDS):
             cols = slice(j * BANK_WORDS, (j + 1) * BANK_WORDS)
@@ -193,9 +208,21 @@ def tile_compute_gate_k_kernel(tc, input_word, hidden_states, Wx, bx, Wh, out_0,
             nc.tensor.matmul(out=spread[:], lhsT=ones[:], rhs=bias_rows[:, cols], start=True, stop=True)
             nc.vector.tensor_copy(out=bias[:, cols], in_=spread[:])
 
-        one_operand_banks(wh_raw[0], None, wh_codes, wh_scales, 0)
+        quantise(h_grouped[:], h_codes[:], h_scales[:])
         load_next_half_pair()
-        one_operand_banks(wh_raw[1], None, wh_codes, wh_scales, HALF_PASSES)
+        wh_jobs = []
+        for b in range(0, BLOCKS, 2):
+            wh_jobs.append(windows(wh_raw, None, b, 0) + windows(wh_raw, None, b + 1, 0))
+
+        wx_firsts = [new_firsts()]
+
+        def after_wh_bank(b):
+            if b == 2:
+                gather_firsts(wx_raw[0], wx_firsts[0], slice(0, BLOCKS_PER_PAIR))
+            if b == 4:
+                move_seconds(wx_raw[0], slice(0, BLOCKS_PER_PAIR))
+
+        prepare(wh_jobs, wh_codes, wh_scales, after_wh_bank)
         load_next_half_pair()
 
         def multiply(n, burst):
@@ -244,35 +271,36 @@ def tile_compute_gate_k_kernel(tc, input_word, hidden_states, Wx, bx, Wh, out_0,
                     func=ACT.Sigmoid if gate == 0 else ACT.Tanh,
                 )
 
-        wx_permuted = [[permute(raw) for raw in wx_raw[0]]]
         for n in range(PAIRS * HALVES):
             i, half = divmod(n, HALVES)
             if half == 0:
                 wx_codes.append(weight_pool.tile([P, X_PASSES * PAIR], U32, name="codes", align_bytes=64))
                 wx_scales.append(weight_pool.tile([P, X_PASSES * PAIR], U8, name="scales", align_bytes=64))
+            wx_jobs = []
             for g in range(HALF_PASSES):
-                stationaries = []
-                for block in range(PAIR // P):
-                    stationaries += windows(wx_raw[n][block], wx_permuted[n][block], g)
-                cols = slice((half * HALF_PASSES + g) * PAIR, (half * HALF_PASSES + g + 1) * PAIR)
-                transpose_bank(stationaries, wx_codes[i][:, cols], wx_scales[i][:, cols])
-                if g == 1 and n > 1:
+                wx_jobs.append(windows(wx_raw[n], wx_firsts[n], 0, g) + windows(wx_raw[n], wx_firsts[n], 1, g))
+
+            def after_wx_bank(b):
+                if b == 0 and n + 1 < PAIRS * HALVES:
+                    wx_firsts.append(new_firsts())
+                    gather_firsts(wx_raw[n + 1], wx_firsts[n + 1], slice(0, BLOCKS_PER_PAIR))
+                if b == 1 and n > 1:
                     add_bias(n - 2)
-                if g == 3 and n > 1:
+                if b == 3 and n > 1:
                     activate(n - 2)
-                if g == 3 and n > 0:
+                if b == 3 and n > 0:
                     multiply(n - 1, 0)
-                if g == 0 and n + 1 < len(wx_raw):
-                    wx_permuted.append([permute(wx_raw[n + 1][0])])
-                if g == 3 and n + 1 < len(wx_raw):
-                    wx_permuted[n + 1].append(permute(wx_raw[n + 1][1]))
-                if g == 7 and n > 0:
+                if b == 4 and n + 1 < PAIRS * HALVES:
+                    move_seconds(wx_raw[n + 1], slice(0, BLOCKS_PER_PAIR))
+                if b == 7 and n > 0:
                     multiply(n - 1, 1)
+
+            cols = slice(half * HALF_PASSES * PAIR, (half + 1) * HALF_PASSES * PAIR)
+            prepare(wx_jobs, wx_codes[i][:, cols], wx_scales[i][:, cols], after_wx_bank)
             load_next_half_pair()
 
         last = PAIRS * HALVES - 1
-        for n in range(len(copied) - QUANTISE_LAG, len(copied)):
-            quantise(n)
+        quantise(*copied.pop(0))
         multiply(last, 0)
         multiply(last, 1)
         add_bias(last)

@@ -22,26 +22,27 @@ GATES = 2
 OUT = CELLS * GATES * H
 X_PASSES = IN // K_PASS
 BLOCKS = OUT // P
+BLOCKS_PER_GATE = H // P
 
 HALVES = 2
 HALF_PASSES = X_PASSES // HALVES
 HALF_K = HALF_PASSES * K_PASS
-BURST = 4
-PAIR = 2 * P
-PAIRS = OUT // PAIR
-PAIRS_PER_GATE = H // PAIR
+QUARTER_PASSES = HALF_PASSES // 2
+QUARTER_K = QUARTER_PASSES * K_PASS
 
 WORDS_PER_PASS = K_PASS // 2
 BANK_WORDS = 512
-RUN = 16
-STRIDED = 2
-MOVED = HALF_PASSES - STRIDED
-BLOCKS_PER_PAIR = PAIR // P
+BANK_PASSES = BANK_WORDS // WORDS_PER_PASS
 QUANTISE_BANKS = 2
+WH_PARTS = 2
+SPLIT_FIRST = 2
+SPLIT_LAST = 1
+RUN = 16
+STRIDED = (1, 0)
 
-VECTOR_COPY_EVERY = 16
+VECTOR_COPY_EVERY = 24
 
-RAW_TILES = 6
+RAW_TILES = 13
 TRANSPOSE_BANKS = 6
 SUM_BANKS = 2
 
@@ -53,58 +54,73 @@ def tile_compute_gate_k_kernel(tc, input_word, hidden_states, Wx, bx, Wh, out_0,
     with ExitStack() as ctx:
         keep = ctx.enter_context(tc.tile_pool(name="keep", bufs=1))
         raw_pool = ctx.enter_context(tc.tile_pool(name="raw", bufs=RAW_TILES))
-        firsts_pool = ctx.enter_context(tc.tile_pool(name="firsts", bufs=2))
+        firsts_pool = ctx.enter_context(tc.tile_pool(name="firsts", bufs=3))
         grouped_pool = ctx.enter_context(tc.tile_pool(name="grouped", bufs=4))
-        weight_pool = ctx.enter_context(tc.tile_pool(name="weight", bufs=2))
+        weight_pool = ctx.enter_context(tc.tile_pool(name="weight", bufs=3))
         out_pool = ctx.enter_context(tc.tile_pool(name="out", bufs=2))
         banks = ctx.enter_context(tc.psum_pool(name="banks", bufs=TRANSPOSE_BANKS))
         sums = ctx.enter_context(tc.psum_pool(name="sums", bufs=SUM_BANKS))
         ctx.enter_context(tc.manual_schedule())
 
-        pair_order = []
+        block_order = []
         for gate in range(GATES):
             for cell in range(CELLS):
-                for part in range(PAIRS_PER_GATE):
-                    pair_order.append((gate, cell, part))
+                for part in range(BLOCKS_PER_GATE):
+                    block_order.append((gate, cell, part))
 
         def net_columns(i):
-            gate, cell, part = pair_order[i]
-            first = (cell * GATES + gate) * H + part * PAIR
-            return slice(first, first + PAIR)
+            gate, cell, part = block_order[i]
+            first = (cell * GATES + gate) * H + part * P
+            return slice(first, first + P)
 
         wx_rows = Wx.rearrange("c n k -> (c n) k")
         wx_raw = []
 
-        def load_next_half_pair():
-            if len(wx_raw) < PAIRS * HALVES:
+        def is_split(n):
+            return n < SPLIT_FIRST or n >= HALVES + BLOCKS * HALVES - SPLIT_LAST
+
+        def load_next():
+            if len(wx_raw) < BLOCKS * HALVES:
                 i, half = divmod(len(wx_raw), HALVES)
-                first = net_columns(i).start
-                raw = raw_pool.tile([P, BLOCKS_PER_PAIR, HALF_K], BF16, name="raw")
-                for block in range(BLOCKS_PER_PAIR):
-                    rows = slice(first + block * P, first + (block + 1) * P)
-                    nc.sync.dma_start(out=raw[:, block, :], in_=wx_rows[rows, half * HALF_K : (half + 1) * HALF_K])
+                raw = raw_pool.tile([P, HALF_K], BF16, name="raw")
+                loads = 2 if is_split(HALVES + len(wx_raw)) else 1
+                for part in range(loads):
+                    n = HALF_K // loads
+                    nc.sync.dma_start(
+                        out=raw[:, part * n : (part + 1) * n],
+                        in_=wx_rows[net_columns(i), half * HALF_K + part * n : half * HALF_K + (part + 1) * n],
+                    )
                 wx_raw.append(raw)
 
-        x_raw = raw_pool.tile([P, HALVES, HALF_K], BF16, name="raw")
-        for half in range(HALVES):
-            for part in range(2):
-                cols = slice(part * HALF_K // 2, (part + 1) * HALF_K // 2)
-                first = half * HALF_K
-                nc.sync.dma_start(
-                    out=x_raw[:, half, cols], in_=input_word[:, first + cols.start : first + cols.stop]
-                )
-        h_raw = keep.tile([P, 1, H], BF16, name="h_raw")
-        nc.sync.dma_start(out=h_raw[:, 0, :], in_=hidden_states)
         bias_rows = keep.tile([P, OUT], BF16, name="bias_rows")
         nc.vector.memset(bias_rows[:].bitcast(I32), 0)
-        nc.sync.dma_start(out=bias_rows[0:1, :], in_=bx.rearrange("(o c) n -> o (c n)", o=1))
         wh_blocks = Wh.rearrange("c (b p) k -> p (c b) k", p=P)
-        wh_raw = raw_pool.tile([P, BLOCKS, K_PASS], BF16, name="raw")
+        wh_raw = []
         for half in range(2):
-            some = slice(half * BLOCKS // 2, (half + 1) * BLOCKS // 2)
-            nc.sync.dma_start(out=wh_raw[:, some, :], in_=wh_blocks[:, some, :])
-        for n in range(RAW_TILES - 2):
-            load_next_half_pair()
+            raw = raw_pool.tile([P, HALF_K], BF16, name="raw")
+            for part in range(WH_PARTS):
+                n = HALF_PASSES // WH_PARTS
+                some = slice(half * HALF_PASSES + part * n, half * HALF_PASSES + (part + 1) * n)
+                nc.sync.dma_start(
+                    out=raw[:, part * n * K_PASS : (part + 1) * n * K_PASS].rearrange("p (b k) -> p b k", k=K_PASS),
+                    in_=wh_blocks[:, some, :],
+                )
+                if half == 0 and part == 0:
+                    nc.sync.dma_start(out=bias_rows[0:1, :], in_=bx.rearrange("(o c) n -> o (c n)", o=1))
+            wh_raw.append(raw)
+        h_raw = keep.tile([P, H], BF16, name="h_raw")
+        nc.sync.dma_start(out=h_raw[:], in_=hidden_states)
+        x_raw = []
+        for half in range(HALVES):
+            raw = raw_pool.tile([P, HALF_K], BF16, name="raw")
+            for part in range(2):
+                first = half * HALF_K + part * QUARTER_K
+                nc.sync.dma_start(
+                    out=raw[:, part * QUARTER_K : (part + 1) * QUARTER_K], in_=input_word[:, first : first + QUARTER_K]
+                )
+            x_raw.append(raw)
+        for n in range(RAW_TILES - 4):
+            load_next()
 
         identity = keep.tile([P, P], F32, name="identity")
         masks.make_identity(nc, identity[:])
@@ -127,27 +143,31 @@ def tile_compute_gate_k_kernel(tc, input_word, hidden_states, Wx, bx, Wh, out_0,
         net_sums = []
         nets = []
 
-        def new_firsts():
-            return firsts_pool.tile([P, 2, MOVED * P * 2], BF16, name="firsts")
+        def new_firsts(half):
+            return firsts_pool.tile([P, 2, (QUARTER_PASSES - STRIDED[half]) * P * 2], BF16, name="firsts")
 
-        def gather_firsts(raw, firsts, blocks):
+        def gather_firsts(raw, half, firsts, quarters):
+            passes = raw[:].rearrange("p (q k) -> p q k", k=QUARTER_K)[:, quarters, STRIDED[half] * K_PASS :]
             nc.vector.tensor_copy(
-                out=firsts[:, blocks, :].rearrange("p k (n s i) -> p k n s i", s=2, i=RUN),
-                in_=raw[:, blocks, STRIDED * K_PASS :].rearrange("p k (s n u i) -> p u k n s i", s=2, u=2, i=RUN)[:, 0],
+                out=firsts[:, quarters, :].rearrange("p q (n s i) -> p q n s i", s=2, i=RUN),
+                in_=passes.rearrange("p q (s n u i) -> p u q n s i", s=2, u=2, i=RUN)[:, 0],
             )
 
-        def move_seconds(raw, blocks):
-            runs = raw[:, blocks, STRIDED * K_PASS :].rearrange("p k (s n u i) -> p s u k n i", s=2, u=2, i=RUN)
+        def move_seconds(raw, half, quarters):
+            passes = raw[:].rearrange("p (q k) -> p q k", k=QUARTER_K)[:, quarters, STRIDED[half] * K_PASS :]
+            runs = passes.rearrange("p q (s n u i) -> p s u q n i", s=2, u=2, i=RUN)
             nc.vector.tensor_copy(out=runs[:, 1, 0], in_=runs[:, 0, 1])
 
-        def windows(raw, firsts, block, g):
-            words = raw[:, block, :].bitcast(F32)
-            if firsts is None or g < STRIDED:
+        def windows(raw, half, firsts, g):
+            words = raw[:].bitcast(F32)
+            q, g_q = divmod(g, QUARTER_PASSES)
+            if firsts is None or g_q < STRIDED[half]:
                 first = g * WORDS_PER_PASS
                 return [words[:, first + u : first + WORDS_PER_PASS : 2] for u in range(2)]
-            first = (g - STRIDED) * P
-            second = STRIDED * WORDS_PER_PASS + MOVED * P + first
-            return [firsts[:, block, :].bitcast(F32)[:, first : first + P], words[:, second : second + P]]
+            moved = QUARTER_PASSES - STRIDED[half]
+            first = (g_q - STRIDED[half]) * P
+            second = (q * QUARTER_PASSES + STRIDED[half]) * WORDS_PER_PASS + moved * P + first
+            return [firsts[:, q, :].bitcast(F32)[:, first : first + P], words[:, second : second + P]]
 
         copied = []
         counts = {"banks": 0}
@@ -168,145 +188,136 @@ def tile_compute_gate_k_kernel(tc, input_word, hidden_states, Wx, bx, Wh, out_0,
                 nc.scalar.copy(out=target, in_=regrouped)
             counts["banks"] += 1
 
-        def prepare(jobs, codes, scales, after_bank):
-            for b, stationaries in enumerate(jobs):
+        def prepare(raw, half, firsts, codes, scales, after_bank):
+            for b in range(HALF_PASSES // BANK_PASSES):
                 width = BANK_WORDS * 2
-                if b % QUANTISE_BANKS == 0:
-                    grouped = grouped_pool.tile([P, QUANTISE_BANKS * width], BF16, name="grouped", align_bytes=64)
                 part = b % QUANTISE_BANKS
+                if part == 0:
+                    grouped = grouped_pool.tile([P, QUANTISE_BANKS * width], BF16, name="grouped", align_bytes=64)
+                stationaries = windows(raw, half, firsts, 2 * b) + windows(raw, half, firsts, 2 * b + 1)
                 transpose_bank(stationaries, grouped[:, part * width : (part + 1) * width])
                 if part == QUANTISE_BANKS - 1:
-                    cols = slice((b - part) * PAIR, (b + 1) * PAIR)
+                    cols = slice((b - part) * BANK_PASSES * P, (b + 1) * BANK_PASSES * P)
                     copied.append((grouped[:], codes[:, cols], scales[:, cols]))
                     if len(copied) > 1:
                         quantise(*copied.pop(0))
                 after_bank(b)
 
-        x_firsts = new_firsts()
+        def spread_bias():
+            for j in range(OUT // BANK_WORDS):
+                cols = slice(j * BANK_WORDS, (j + 1) * BANK_WORDS)
+                spread = banks.tile([P, BANK_WORDS], F32, name="bank")
+                nc.tensor.matmul(out=spread[:], lhsT=ones[:], rhs=bias_rows[:, cols], start=True, stop=True)
+                nc.vector.tensor_copy(out=bias[:, cols], in_=spread[:])
 
-        def move_x(half):
-            gather_firsts(x_raw, x_firsts, slice(half, half + 1))
-            move_seconds(x_raw, slice(half, half + 1))
+        firsts = {}
 
-        def after_x_bank(b):
-            if b == 2:
-                move_x(1)
+        def raw_tile(n):
+            return x_raw[n] if n < HALVES else wx_raw[n - HALVES]
 
-        x_jobs = []
-        for g in range(0, X_PASSES, 2):
-            half, first = divmod(g, HALF_PASSES)
-            x_jobs.append(windows(x_raw, x_firsts, half, first) + windows(x_raw, x_firsts, half, first + 1))
-        move_x(0)
-        prepare(x_jobs, x_codes, x_scales, after_x_bank)
+        def move(n, b):
+            if n < HALVES + BLOCKS * HALVES:
+                half = n % HALVES
+                if is_split(n):
+                    if b == 0:
+                        firsts[n] = new_firsts(half)
+                    if b < 2:
+                        gather_firsts(raw_tile(n), half, firsts[n], slice(b, b + 1))
+                        move_seconds(raw_tile(n), half, slice(b, b + 1))
+                else:
+                    if b == 0:
+                        firsts[n] = new_firsts(half)
+                        gather_firsts(raw_tile(n), half, firsts[n], slice(0, 2))
+                    if b == 1:
+                        move_seconds(raw_tile(n), half, slice(0, 2))
+
+        def nothing(b):
+            return
+
         h_grouped = keep.tile([P, H], BF16, name="h_grouped", align_bytes=64)
-        transpose_bank(windows(h_raw, None, 0, 0), h_grouped[:])
-        quantise(*copied.pop(0))
-
-        for j in range(OUT // BANK_WORDS):
-            cols = slice(j * BANK_WORDS, (j + 1) * BANK_WORDS)
-            spread = banks.tile([P, BANK_WORDS], F32, name="bank")
-            nc.tensor.matmul(out=spread[:], lhsT=ones[:], rhs=bias_rows[:, cols], start=True, stop=True)
-            nc.vector.tensor_copy(out=bias[:, cols], in_=spread[:])
-
+        for half in range(2):
+            cols = slice(half * HALF_PASSES * P, (half + 1) * HALF_PASSES * P)
+            if half == 1:
+                transpose_bank(windows(h_raw, 0, None, 0), h_grouped[:])
+            prepare(wh_raw[half], half, None, wh_codes[:, cols], wh_scales[:, cols], (lambda b: move(0, b)) if half == 1 else nothing)
+            load_next()
+            if half == 0:
+                spread_bias()
         quantise(h_grouped[:], h_codes[:], h_scales[:])
-        load_next_half_pair()
-        wh_jobs = []
-        for b in range(0, BLOCKS, 2):
-            wh_jobs.append(windows(wh_raw, None, b, 0) + windows(wh_raw, None, b + 1, 0))
+        for half in range(HALVES):
+            cols = slice(half * HALF_PASSES * P, (half + 1) * HALF_PASSES * P)
+            prepare(x_raw[half], half, firsts[half], x_codes[:, cols], x_scales[:, cols], lambda b: move(half + 1, b))
+            load_next()
 
-        wx_firsts = [new_firsts()]
-
-        def after_wh_bank(b):
-            if b == 2:
-                gather_firsts(wx_raw[0], wx_firsts[0], slice(0, BLOCKS_PER_PAIR))
-            if b == 4:
-                move_seconds(wx_raw[0], slice(0, BLOCKS_PER_PAIR))
-
-        prepare(wh_jobs, wh_codes, wh_scales, after_wh_bank)
-        load_next_half_pair()
-
-        def multiply(n, burst):
-            i, half = divmod(n, HALVES)
-            if half == 0 and burst == 0:
+        def multiply(m):
+            i, half = divmod(m, HALVES)
+            if half == 0:
                 net_sums.append(sums.tile([P, BANK_WORDS], F32, name="acc"))
-            acc = net_sums[i][:, :PAIR]
-            first = half * HALF_PASSES + burst * BURST
-            for g in range(first, first + BURST):
-                x_cols = slice(g * P, (g + 1) * P)
-                w_cols = slice(g * PAIR, (g + 1) * PAIR)
                 nc.tensor.matmul_mx(
-                    out=acc,
-                    lhsT=x_codes[:, x_cols].bitcast(FP8X4),
-                    lhsT_scale=x_scales[:, x_cols],
-                    rhs=wx_codes[i][:, w_cols].bitcast(FP8X4),
-                    rhs_scale=wx_scales[i][:, w_cols],
-                    start=(g == 0),
-                    stop=False,
-                )
-            if first + BURST == X_PASSES:
-                nc.tensor.matmul_mx(
-                    out=acc,
+                    out=net_sums[i][:, :P],
                     lhsT=h_codes[:].bitcast(FP8X4),
                     lhsT_scale=h_scales[:],
                     rhs=wh_codes[:, net_columns(i)].bitcast(FP8X4),
                     rhs_scale=wh_scales[:, net_columns(i)],
+                    start=True,
+                    stop=False,
+                )
+            for g in range(half * HALF_PASSES, (half + 1) * HALF_PASSES):
+                cols = slice(g * P, (g + 1) * P)
+                nc.tensor.matmul_mx(
+                    out=net_sums[i][:, :P],
+                    lhsT=x_codes[:, cols].bitcast(FP8X4),
+                    lhsT_scale=x_scales[:, cols],
+                    rhs=wx_codes[i][:, cols].bitcast(FP8X4),
+                    rhs_scale=wx_scales[i][:, cols],
                     start=False,
-                    stop=True,
+                    stop=(g == X_PASSES - 1),
                 )
 
-        def add_bias(n):
-            i, half = divmod(n, HALVES)
-            if half == HALVES - 1:
-                net = out_pool.tile([P, PAIR], F32, name="net")
-                nc.vector.tensor_tensor(out=net[:], in0=net_sums[i][:, :PAIR], in1=bias[:, net_columns(i)], op=ALU.add)
-                nets.append(net)
+        def add_bias(i):
+            net = out_pool.tile([P, P], F32, name="net")
+            nc.vector.tensor_tensor(out=net[:], in0=net_sums[i][:, :P], in1=bias[:, net_columns(i)], op=ALU.add)
+            nets.append(net)
 
-        def activate(n):
-            i, half = divmod(n, HALVES)
-            if half == HALVES - 1:
-                gate, cell, part = pair_order[i]
-                nc.scalar.activation(
-                    out=results[:, i // PAIRS_PER_GATE, part * PAIR : (part + 1) * PAIR],
-                    in_=nets[i][:],
-                    func=ACT.Sigmoid if gate == 0 else ACT.Tanh,
-                )
+        def activate(i):
+            gate, cell, part = block_order[i]
+            nc.scalar.activation(
+                out=results[:, i // BLOCKS_PER_GATE, part * P : (part + 1) * P],
+                in_=nets[i][:],
+                func=ACT.Sigmoid if gate == 0 else ACT.Tanh,
+            )
 
-        for n in range(PAIRS * HALVES):
-            i, half = divmod(n, HALVES)
+        def prepare_wx(m):
+            i, half = divmod(m, HALVES)
             if half == 0:
-                wx_codes.append(weight_pool.tile([P, X_PASSES * PAIR], U32, name="codes", align_bytes=64))
-                wx_scales.append(weight_pool.tile([P, X_PASSES * PAIR], U8, name="scales", align_bytes=64))
-            wx_jobs = []
-            for g in range(HALF_PASSES):
-                wx_jobs.append(windows(wx_raw[n], wx_firsts[n], 0, g) + windows(wx_raw[n], wx_firsts[n], 1, g))
+                wx_codes.append(weight_pool.tile([P, X_PASSES * P], U32, name="codes", align_bytes=64))
+                wx_scales.append(weight_pool.tile([P, X_PASSES * P], U8, name="scales", align_bytes=64))
 
-            def after_wx_bank(b):
-                if b == 0 and n + 1 < PAIRS * HALVES:
-                    wx_firsts.append(new_firsts())
-                    gather_firsts(wx_raw[n + 1], wx_firsts[n + 1], slice(0, BLOCKS_PER_PAIR))
-                if b == 1 and n > 1:
-                    add_bias(n - 2)
-                if b == 3 and n > 1:
-                    activate(n - 2)
-                if b == 3 and n > 0:
-                    multiply(n - 1, 0)
-                if b == 4 and n + 1 < PAIRS * HALVES:
-                    move_seconds(wx_raw[n + 1], slice(0, BLOCKS_PER_PAIR))
-                if b == 7 and n > 0:
-                    multiply(n - 1, 1)
+            def after_bank(b):
+                move(HALVES + m + 1, b)
+                if b == 1 and half == 1 and i > 0:
+                    add_bias(i - 1)
+                if b == 3 and half == 1 and i > 0:
+                    activate(i - 1)
+                if b == 3 and m > 0:
+                    multiply(m - 1)
 
-            cols = slice(half * HALF_PASSES * PAIR, (half + 1) * HALF_PASSES * PAIR)
-            prepare(wx_jobs, wx_codes[i][:, cols], wx_scales[i][:, cols], after_wx_bank)
-            load_next_half_pair()
+            cols = slice(half * HALF_PASSES * P, (half + 1) * HALF_PASSES * P)
+            prepare(wx_raw[m], half, firsts[HALVES + m], wx_codes[i][:, cols], wx_scales[i][:, cols], after_bank)
+            load_next()
 
-        last = PAIRS * HALVES - 1
+        for m in range(BLOCKS * HALVES):
+            prepare_wx(m)
         quantise(*copied.pop(0))
-        multiply(last, 0)
-        multiply(last, 1)
-        add_bias(last)
-        activate(last)
+        multiply(BLOCKS * HALVES - 1)
+        add_bias(BLOCKS - 1)
+        activate(BLOCKS - 1)
 
-        for j in range(GATES * CELLS):
-            gate, cell, part = pair_order[j * PAIRS_PER_GATE]
+        for i in range(0, BLOCKS, BLOCKS_PER_GATE):
+            gate, cell, part = block_order[i]
             out = out_1 if gate == 0 else out_0
-            nc.sync.dma_start(out=out[:, cell, :], in_=results[:, j, :])
+            cuts = (0, H) if i + BLOCKS_PER_GATE < BLOCKS else (0, H - P, H)
+            for first, end in zip(cuts, cuts[1:]):
+                nc.sync.dma_start(
+                    out=out[:, cell, first:end], in_=results[:, i // BLOCKS_PER_GATE, first:end]
+                )

@@ -22,25 +22,29 @@ GATES = 2
 OUT = CELLS * GATES * H
 X_PASSES = IN // K_PASS
 BLOCKS = OUT // P
-BLOCKS_PER_GATE = H // P
+PAIR = 2 * P
+PAIRS = OUT // PAIR
+PAIRS_PER_GATE = H // PAIR
 
-HALVES = 2
-HALF_PASSES = X_PASSES // HALVES
-HALF_K = HALF_PASSES * K_PASS
-QUARTER_PASSES = HALF_PASSES // 2
+QUARTERS = 4
+QUARTER_PASSES = X_PASSES // QUARTERS
 QUARTER_K = QUARTER_PASSES * K_PASS
 
 WORDS_PER_PASS = K_PASS // 2
 BANK_WORDS = 512
 BANK_PASSES = BANK_WORDS // WORDS_PER_PASS
 QUANTISE_BANKS = 2
-WH_PARTS = 2
-SPLIT_FIRST = 2
-SPLIT_LAST = 1
+WH_PARTS = 4
 RUN = 16
-STRIDED = (1, 0)
+STRIDED = (1, 1, 1, 1)
+NEAR = 4
+BIAS_AFTER_WH = ((0,), (1,))
+BIAS_AFTER_X = ((2,), (3,))
+BIAS_SCALAR = ()
+BURST = 2
+MULTIPLY_LAG = 2
 
-VECTOR_COPY_EVERY = 24
+VECTOR_COPY_EVERY = 14
 
 RAW_TILES = 13
 TRANSPOSE_BANKS = 6
@@ -54,71 +58,58 @@ def tile_compute_gate_k_kernel(tc, input_word, hidden_states, Wx, bx, Wh, out_0,
     with ExitStack() as ctx:
         keep = ctx.enter_context(tc.tile_pool(name="keep", bufs=1))
         raw_pool = ctx.enter_context(tc.tile_pool(name="raw", bufs=RAW_TILES))
-        firsts_pool = ctx.enter_context(tc.tile_pool(name="firsts", bufs=3))
+        firsts_pool = ctx.enter_context(tc.tile_pool(name="firsts", bufs=4))
         grouped_pool = ctx.enter_context(tc.tile_pool(name="grouped", bufs=4))
-        weight_pool = ctx.enter_context(tc.tile_pool(name="weight", bufs=3))
+        weight_pool = ctx.enter_context(tc.tile_pool(name="weight", bufs=2))
         out_pool = ctx.enter_context(tc.tile_pool(name="out", bufs=2))
         banks = ctx.enter_context(tc.psum_pool(name="banks", bufs=TRANSPOSE_BANKS))
         sums = ctx.enter_context(tc.psum_pool(name="sums", bufs=SUM_BANKS))
         ctx.enter_context(tc.manual_schedule())
 
-        block_order = []
+        pair_order = []
         for gate in range(GATES):
             for cell in range(CELLS):
-                for part in range(BLOCKS_PER_GATE):
-                    block_order.append((gate, cell, part))
+                for part in range(PAIRS_PER_GATE):
+                    pair_order.append((gate, cell, part))
 
         def net_columns(i):
-            gate, cell, part = block_order[i]
-            first = (cell * GATES + gate) * H + part * P
-            return slice(first, first + P)
+            gate, cell, part = pair_order[i]
+            first = (cell * GATES + gate) * H + part * PAIR
+            return slice(first, first + PAIR)
 
         wx_rows = Wx.rearrange("c n k -> (c n) k")
         wx_raw = []
 
-        def is_split(n):
-            return n < SPLIT_FIRST or n >= HALVES + BLOCKS * HALVES - SPLIT_LAST
-
         def load_next():
-            if len(wx_raw) < BLOCKS * HALVES:
-                i, half = divmod(len(wx_raw), HALVES)
-                raw = raw_pool.tile([P, HALF_K], BF16, name="raw")
-                loads = 2 if is_split(HALVES + len(wx_raw)) else 1
-                for part in range(loads):
-                    n = HALF_K // loads
-                    nc.sync.dma_start(
-                        out=raw[:, part * n : (part + 1) * n],
-                        in_=wx_rows[net_columns(i), half * HALF_K + part * n : half * HALF_K + (part + 1) * n],
-                    )
+            if len(wx_raw) < PAIRS * QUARTERS:
+                i, part = divmod(len(wx_raw), QUARTERS)
+                raw = raw_pool.tile([P, 2, QUARTER_K], BF16, name="raw")
+                rows = wx_rows[net_columns(i), :].rearrange("(b p) k -> p b k", p=P)
+                nc.sync.dma_start(out=raw[:], in_=rows[:, :, part * QUARTER_K : (part + 1) * QUARTER_K])
                 wx_raw.append(raw)
 
         bias_rows = keep.tile([P, OUT], BF16, name="bias_rows")
         nc.vector.memset(bias_rows[:].bitcast(I32), 0)
         wh_blocks = Wh.rearrange("c (b p) k -> p (c b) k", p=P)
         wh_raw = []
-        for half in range(2):
-            raw = raw_pool.tile([P, HALF_K], BF16, name="raw")
-            for part in range(WH_PARTS):
-                n = HALF_PASSES // WH_PARTS
-                some = slice(half * HALF_PASSES + part * n, half * HALF_PASSES + (part + 1) * n)
-                nc.sync.dma_start(
-                    out=raw[:, part * n * K_PASS : (part + 1) * n * K_PASS].rearrange("p (b k) -> p b k", k=K_PASS),
-                    in_=wh_blocks[:, some, :],
-                )
-                if half == 0 and part == 0:
-                    nc.sync.dma_start(out=bias_rows[0:1, :], in_=bx.rearrange("(o c) n -> o (c n)", o=1))
-            wh_raw.append(raw)
+        for part in range(WH_PARTS):
+            n = BLOCKS // WH_PARTS
+            if part % 2 == 0:
+                raw = raw_pool.tile([P, 2, QUARTER_K], BF16, name="raw")
+                wh_raw.append(raw)
+            nc.sync.dma_start(
+                out=raw[:, part % 2, :].rearrange("p (b k) -> p b k", k=K_PASS), in_=wh_blocks[:, part * n : (part + 1) * n, :]
+            )
+            if part == 0:
+                nc.sync.dma_start(out=bias_rows[0:1, :], in_=bx.rearrange("(o c) n -> o (c n)", o=1))
         h_raw = keep.tile([P, H], BF16, name="h_raw")
         nc.sync.dma_start(out=h_raw[:], in_=hidden_states)
         x_raw = []
-        for half in range(HALVES):
-            raw = raw_pool.tile([P, HALF_K], BF16, name="raw")
-            for part in range(2):
-                first = half * HALF_K + part * QUARTER_K
-                nc.sync.dma_start(
-                    out=raw[:, part * QUARTER_K : (part + 1) * QUARTER_K], in_=input_word[:, first : first + QUARTER_K]
-                )
-            x_raw.append(raw)
+        for part in range(QUARTERS):
+            if part % 2 == 0:
+                raw = raw_pool.tile([P, 2, QUARTER_K], BF16, name="raw")
+            nc.sync.dma_start(out=raw[:, part % 2, :], in_=input_word[:, part * QUARTER_K : (part + 1) * QUARTER_K])
+            x_raw.append(raw[:, part % 2 : part % 2 + 1, :])
         for n in range(RAW_TILES - 4):
             load_next()
 
@@ -143,31 +134,31 @@ def tile_compute_gate_k_kernel(tc, input_word, hidden_states, Wx, bx, Wh, out_0,
         net_sums = []
         nets = []
 
-        def new_firsts(half):
-            return firsts_pool.tile([P, 2, (QUARTER_PASSES - STRIDED[half]) * P * 2], BF16, name="firsts")
-
-        def gather_firsts(raw, half, firsts, quarters):
-            passes = raw[:].rearrange("p (q k) -> p q k", k=QUARTER_K)[:, quarters, STRIDED[half] * K_PASS :]
+        def gather_firsts(raw, part):
+            blocks = raw.shape[1]
+            firsts = firsts_pool.tile([P, blocks, (QUARTER_PASSES - STRIDED[part]) * P * 2], BF16, name="firsts")
+            words = raw[:, :, STRIDED[part] * K_PASS :]
             nc.vector.tensor_copy(
-                out=firsts[:, quarters, :].rearrange("p q (n s i) -> p q n s i", s=2, i=RUN),
-                in_=passes.rearrange("p q (s n u i) -> p u q n s i", s=2, u=2, i=RUN)[:, 0],
+                out=firsts[:].rearrange("p k (n s i) -> p k n s i", s=2, i=RUN),
+                in_=words.rearrange("p k (s n u i) -> p u k n s i", s=2, u=2, i=RUN)[:, 0],
             )
+            return firsts
 
-        def move_seconds(raw, half, quarters):
-            passes = raw[:].rearrange("p (q k) -> p q k", k=QUARTER_K)[:, quarters, STRIDED[half] * K_PASS :]
-            runs = passes.rearrange("p q (s n u i) -> p s u q n i", s=2, u=2, i=RUN)
+        def move_seconds(raw, part):
+            words = raw[:, :, STRIDED[part] * K_PASS :]
+            runs = words.rearrange("p k (s n u i) -> p s u k n i", s=2, u=2, i=RUN)
             nc.vector.tensor_copy(out=runs[:, 1, 0], in_=runs[:, 0, 1])
 
-        def windows(raw, half, firsts, g):
-            words = raw[:].bitcast(F32)
-            q, g_q = divmod(g, QUARTER_PASSES)
-            if firsts is None or g_q < STRIDED[half]:
-                first = g * WORDS_PER_PASS
-                return [words[:, first + u : first + WORDS_PER_PASS : 2] for u in range(2)]
-            moved = QUARTER_PASSES - STRIDED[half]
-            first = (g_q - STRIDED[half]) * P
-            second = (q * QUARTER_PASSES + STRIDED[half]) * WORDS_PER_PASS + moved * P + first
-            return [firsts[:, q, :].bitcast(F32)[:, first : first + P], words[:, second : second + P]]
+        def strided_windows(words):
+            return [words[:, u::2] for u in range(2)]
+
+        def windows(raw, part, firsts, block, g):
+            words = raw[:, block, :].bitcast(F32)
+            if g < STRIDED[part]:
+                return strided_windows(words[:, g * WORDS_PER_PASS : (g + 1) * WORDS_PER_PASS])
+            first = (g - STRIDED[part]) * P
+            second = STRIDED[part] * WORDS_PER_PASS + (QUARTER_PASSES - STRIDED[part]) * P + first
+            return [firsts[:, block, :].bitcast(F32)[:, first : first + P], words[:, second : second + P]]
 
         copied = []
         counts = {"banks": 0}
@@ -188,73 +179,73 @@ def tile_compute_gate_k_kernel(tc, input_word, hidden_states, Wx, bx, Wh, out_0,
                 nc.scalar.copy(out=target, in_=regrouped)
             counts["banks"] += 1
 
-        def prepare(raw, half, firsts, codes, scales, after_bank):
-            for b in range(HALF_PASSES // BANK_PASSES):
+        def prepare(jobs, codes, scales, after_bank):
+            for b, stationaries in enumerate(jobs):
                 width = BANK_WORDS * 2
                 part = b % QUANTISE_BANKS
                 if part == 0:
                     grouped = grouped_pool.tile([P, QUANTISE_BANKS * width], BF16, name="grouped", align_bytes=64)
-                stationaries = windows(raw, half, firsts, 2 * b) + windows(raw, half, firsts, 2 * b + 1)
                 transpose_bank(stationaries, grouped[:, part * width : (part + 1) * width])
                 if part == QUANTISE_BANKS - 1:
-                    cols = slice((b - part) * BANK_PASSES * P, (b + 1) * BANK_PASSES * P)
+                    cols = slice((b - part) * PAIR, (b + 1) * PAIR)
                     copied.append((grouped[:], codes[:, cols], scales[:, cols]))
                     if len(copied) > 1:
                         quantise(*copied.pop(0))
                 after_bank(b)
 
-        def spread_bias():
-            for j in range(OUT // BANK_WORDS):
-                cols = slice(j * BANK_WORDS, (j + 1) * BANK_WORDS)
-                spread = banks.tile([P, BANK_WORDS], F32, name="bank")
-                nc.tensor.matmul(out=spread[:], lhsT=ones[:], rhs=bias_rows[:, cols], start=True, stop=True)
+        def spread_bias(j):
+            cols = slice(j * BANK_WORDS, (j + 1) * BANK_WORDS)
+            spread = banks.tile([P, BANK_WORDS], F32, name="bank")
+            nc.tensor.matmul(out=spread[:], lhsT=ones[:], rhs=bias_rows[:, cols], start=True, stop=True)
+            if j in BIAS_SCALAR:
+                nc.scalar.copy(out=bias[:, cols], in_=spread[:])
+            else:
                 nc.vector.tensor_copy(out=bias[:, cols], in_=spread[:])
 
         firsts = {}
 
-        def raw_tile(n):
-            return x_raw[n] if n < HALVES else wx_raw[n - HALVES]
-
         def move(n, b):
-            if n < HALVES + BLOCKS * HALVES:
-                half = n % HALVES
-                if is_split(n):
-                    if b == 0:
-                        firsts[n] = new_firsts(half)
-                    if b < 2:
-                        gather_firsts(raw_tile(n), half, firsts[n], slice(b, b + 1))
-                        move_seconds(raw_tile(n), half, slice(b, b + 1))
-                else:
-                    if b == 0:
-                        firsts[n] = new_firsts(half)
-                        gather_firsts(raw_tile(n), half, firsts[n], slice(0, 2))
-                    if b == 1:
-                        move_seconds(raw_tile(n), half, slice(0, 2))
-
-        def nothing(b):
-            return
+            if n < QUARTERS + PAIRS * QUARTERS:
+                raw = x_raw[n] if n < QUARTERS else wx_raw[n - QUARTERS][:]
+                if b == 0:
+                    firsts[n] = gather_firsts(raw, n % QUARTERS)
+                if b == 1:
+                    move_seconds(raw, n % QUARTERS)
 
         h_grouped = keep.tile([P, H], BF16, name="h_grouped", align_bytes=64)
         for half in range(2):
-            cols = slice(half * HALF_PASSES * P, (half + 1) * HALF_PASSES * P)
+            cols = slice(half * OUT // 2, (half + 1) * OUT // 2)
+            jobs = []
+            for b in range(0, BLOCKS // 2, 2):
+                passes = wh_raw[half][:].rearrange("p k (b w) -> p (k b) w", w=K_PASS)
+                jobs.append(
+                    strided_windows(passes[:, b, :].bitcast(F32)) + strided_windows(passes[:, b + 1, :].bitcast(F32))
+                )
+            prepare(jobs, wh_codes[:, cols], wh_scales[:, cols], (lambda b: move(0, b - 2)) if half == 1 else (lambda b: None))
+            load_next()
+            for j in BIAS_AFTER_WH[half]:
+                spread_bias(j)
             if half == 1:
-                transpose_bank(windows(h_raw, 0, None, 0), h_grouped[:])
-            prepare(wh_raw[half], half, None, wh_codes[:, cols], wh_scales[:, cols], (lambda b: move(0, b)) if half == 1 else nothing)
-            load_next()
-            if half == 0:
-                spread_bias()
+                transpose_bank(strided_windows(h_raw[:].bitcast(F32)), h_grouped[:])
         quantise(h_grouped[:], h_codes[:], h_scales[:])
-        for half in range(HALVES):
-            cols = slice(half * HALF_PASSES * P, (half + 1) * HALF_PASSES * P)
-            prepare(x_raw[half], half, firsts[half], x_codes[:, cols], x_scales[:, cols], lambda b: move(half + 1, b))
-            load_next()
+        for part in range(QUARTERS):
+            raw = x_raw[part]
+            cols = slice(part * QUARTER_PASSES * P, (part + 1) * QUARTER_PASSES * P)
+            jobs = []
+            for g in range(0, QUARTER_PASSES, 2):
+                jobs.append(windows(raw, part, firsts[part], 0, g) + windows(raw, part, firsts[part], 0, g + 1))
+            prepare(jobs, x_codes[:, cols], x_scales[:, cols], lambda b: move(part + 1, b))
+            if part % 2 == 1:
+                load_next()
+                for j in BIAS_AFTER_X[part // 2]:
+                    spread_bias(j)
 
         def multiply(m):
-            i, half = divmod(m, HALVES)
-            if half == 0:
+            i, part = divmod(m, QUARTERS)
+            if part == 0:
                 net_sums.append(sums.tile([P, BANK_WORDS], F32, name="acc"))
                 nc.tensor.matmul_mx(
-                    out=net_sums[i][:, :P],
+                    out=net_sums[i][:, :PAIR],
                     lhsT=h_codes[:].bitcast(FP8X4),
                     lhsT_scale=h_scales[:],
                     rhs=wh_codes[:, net_columns(i)].bitcast(FP8X4),
@@ -262,62 +253,80 @@ def tile_compute_gate_k_kernel(tc, input_word, hidden_states, Wx, bx, Wh, out_0,
                     start=True,
                     stop=False,
                 )
-            for g in range(half * HALF_PASSES, (half + 1) * HALF_PASSES):
-                cols = slice(g * P, (g + 1) * P)
+            for g in range(part * QUARTER_PASSES, (part + 1) * QUARTER_PASSES):
+                x_cols = slice(g * P, (g + 1) * P)
+                w_cols = slice(g * PAIR, (g + 1) * PAIR)
                 nc.tensor.matmul_mx(
-                    out=net_sums[i][:, :P],
-                    lhsT=x_codes[:, cols].bitcast(FP8X4),
-                    lhsT_scale=x_scales[:, cols],
-                    rhs=wx_codes[i][:, cols].bitcast(FP8X4),
-                    rhs_scale=wx_scales[i][:, cols],
+                    out=net_sums[i][:, :PAIR],
+                    lhsT=x_codes[:, x_cols].bitcast(FP8X4),
+                    lhsT_scale=x_scales[:, x_cols],
+                    rhs=wx_codes[i][:, w_cols].bitcast(FP8X4),
+                    rhs_scale=wx_scales[i][:, w_cols],
                     start=False,
                     stop=(g == X_PASSES - 1),
                 )
 
         def add_bias(i):
-            net = out_pool.tile([P, P], F32, name="net")
-            nc.vector.tensor_tensor(out=net[:], in0=net_sums[i][:, :P], in1=bias[:, net_columns(i)], op=ALU.add)
+            net = out_pool.tile([P, PAIR], F32, name="net")
+            nc.vector.tensor_tensor(out=net[:], in0=net_sums[i][:, :PAIR], in1=bias[:, net_columns(i)], op=ALU.add)
             nets.append(net)
 
         def activate(i):
-            gate, cell, part = block_order[i]
+            gate, cell, part = pair_order[i]
             nc.scalar.activation(
-                out=results[:, i // BLOCKS_PER_GATE, part * P : (part + 1) * P],
+                out=results[:, i // PAIRS_PER_GATE, part * PAIR : (part + 1) * PAIR],
                 in_=nets[i][:],
                 func=ACT.Sigmoid if gate == 0 else ACT.Tanh,
             )
 
+        last = PAIRS * QUARTERS - 1
+        ended = [0, 0, 0]
+
         def prepare_wx(m):
-            i, half = divmod(m, HALVES)
-            if half == 0:
-                wx_codes.append(weight_pool.tile([P, X_PASSES * P], U32, name="codes", align_bytes=64))
-                wx_scales.append(weight_pool.tile([P, X_PASSES * P], U8, name="scales", align_bytes=64))
+            i, part = divmod(m, QUARTERS)
+            if part == 0:
+                wx_codes.append(weight_pool.tile([P, X_PASSES * PAIR], U32, name="codes", align_bytes=64))
+                wx_scales.append(weight_pool.tile([P, X_PASSES * PAIR], U8, name="scales", align_bytes=64))
+            raw = wx_raw[m]
 
             def after_bank(b):
-                move(HALVES + m + 1, b)
-                if b == 1 and half == 1 and i > 0:
-                    add_bias(i - 1)
-                if b == 3 and half == 1 and i > 0:
-                    activate(i - 1)
-                if b == 3 and m > 0:
-                    multiply(m - 1)
+                if m < NEAR:
+                    move(QUARTERS + m + 1, b)
+                if m >= NEAR - 1:
+                    move(QUARTERS + m + 2, b - 2)
+                if b == 1 and ended[1] < ended[0] // QUARTERS:
+                    add_bias(ended[1])
+                    ended[1] += 1
+                if b == 3 and ended[2] < ended[1]:
+                    activate(ended[2])
+                    ended[2] += 1
+                if b == 3 and m >= MULTIPLY_LAG and (m - MULTIPLY_LAG) % BURST == BURST - 1:
+                    while ended[0] <= m - MULTIPLY_LAG:
+                        multiply(ended[0])
+                        ended[0] += 1
 
-            cols = slice(half * HALF_PASSES * P, (half + 1) * HALF_PASSES * P)
-            prepare(wx_raw[m], half, firsts[HALVES + m], wx_codes[i][:, cols], wx_scales[i][:, cols], after_bank)
+            jobs = []
+            for g in range(QUARTER_PASSES):
+                jobs.append(
+                    windows(raw, part, firsts[QUARTERS + m], 0, g) + windows(raw, part, firsts[QUARTERS + m], 1, g)
+                )
+            cols = slice(part * QUARTER_PASSES * PAIR, (part + 1) * QUARTER_PASSES * PAIR)
+            prepare(jobs, wx_codes[i][:, cols], wx_scales[i][:, cols], after_bank)
             load_next()
 
-        for m in range(BLOCKS * HALVES):
+        for m in range(PAIRS * QUARTERS):
             prepare_wx(m)
         quantise(*copied.pop(0))
-        multiply(BLOCKS * HALVES - 1)
-        add_bias(BLOCKS - 1)
-        activate(BLOCKS - 1)
+        for m in range(ended[0], last + 1):
+            multiply(m)
+        add_bias(PAIRS - 1)
+        activate(PAIRS - 1)
 
-        for i in range(0, BLOCKS, BLOCKS_PER_GATE):
-            gate, cell, part = block_order[i]
+        for i in range(0, PAIRS, PAIRS_PER_GATE):
+            gate, cell, part = pair_order[i]
             out = out_1 if gate == 0 else out_0
-            cuts = (0, H) if i + BLOCKS_PER_GATE < BLOCKS else (0, H - P, H)
+            cuts = (0, H) if i + PAIRS_PER_GATE < PAIRS else (0, H - PAIR, H)
             for first, end in zip(cuts, cuts[1:]):
                 nc.sync.dma_start(
-                    out=out[:, cell, first:end], in_=results[:, i // BLOCKS_PER_GATE, first:end]
+                    out=out[:, cell, first:end], in_=results[:, i // PAIRS_PER_GATE, first:end]
                 )

@@ -171,8 +171,8 @@ def tile_compute_gate_k_kernel(tc, input_word, hidden_states, Wx, bx, Wh, out_0,
             for i, stationary in enumerate(stationaries):
                 nc.tensor.transpose(bank[:, i * P : (i + 1) * P], stationary, identity[:])
             width = len(stationaries) * P
-            regrouped = bank[:, :width].rearrange("p (g u r) -> p g r u", u=2, r=P)
-            target = grouped.bitcast(F32).rearrange("p (g r u) -> p g r u", u=2, r=P)
+            regrouped = bank[:, :width].rearrange("p (g u r i) -> p g r u i", u=2, i=2, r=P // 2)
+            target = grouped.bitcast(F32).rearrange("p (g r i u) -> p g r u i", u=2, i=2, r=P // 2)
             if counts["banks"] % VECTOR_COPY_EVERY == VECTOR_COPY_EVERY - 1:
                 nc.vector.tensor_copy(out=target, in_=regrouped)
             else:

@@ -38,8 +38,12 @@ WH_PARTS = 4
 RUN = 16
 STRIDED = (1, 1, 1, 1)
 NEAR = 4
+WH_V = ()
+WH_CUTS = (0, 4, 8, 12, 16)
+LAST_V = (2,)
+LAST_Q = 1
 BIAS_AFTER_WH = ((0,), (1,))
-BIAS_AFTER_X = ((2,), (3,))
+BIAS_AFTER_X = ((), ())
 BIAS_SCALAR = ()
 BURST = 2
 MULTIPLY_LAG = 2
@@ -83,7 +87,7 @@ def tile_compute_gate_k_kernel(tc, input_word, hidden_states, Wx, bx, Wh, out_0,
         def load_next():
             if len(wx_raw) < PAIRS * QUARTERS:
                 i, part = divmod(len(wx_raw), QUARTERS)
-                raw = raw_pool.tile([P, 2, QUARTER_K], BF16, name="raw")
+                raw = raw_pool.tile([P, 2, QUARTER_K], BF16, name="raw", align_bytes=512)
                 rows = wx_rows[net_columns(i), :].rearrange("(b p) k -> p b k", p=P)
                 nc.sync.dma_start(out=raw[:], in_=rows[:, :, part * QUARTER_K : (part + 1) * QUARTER_K])
                 wx_raw.append(raw)
@@ -92,28 +96,26 @@ def tile_compute_gate_k_kernel(tc, input_word, hidden_states, Wx, bx, Wh, out_0,
         nc.vector.memset(bias_rows[:].bitcast(I32), 0)
         wh_blocks = Wh.rearrange("c (b p) k -> p (c b) k", p=P)
         wh_raw = []
-        for part in range(WH_PARTS):
-            n = BLOCKS // WH_PARTS
-            if part % 2 == 0:
-                raw = raw_pool.tile([P, 2, QUARTER_K], BF16, name="raw")
-                wh_raw.append(raw)
-            nc.sync.dma_start(
-                out=raw[:, part % 2, :].rearrange("p (b k) -> p b k", k=K_PASS), in_=wh_blocks[:, part * n : (part + 1) * n, :]
-            )
-            if part == 0:
+        for part in range(2):
+            wh_raw.append(raw_pool.tile([P, 2, QUARTER_K], BF16, name="raw", align_bytes=512))
+        for first, end in zip(WH_CUTS, WH_CUTS[1:]):
+            half, b = divmod(first, BLOCKS // 2)
+            raw = wh_raw[half][:].rearrange("p a (b k) -> p (a b) k", k=K_PASS)
+            nc.sync.dma_start(out=raw[:, b : b + end - first, :], in_=wh_blocks[:, first:end, :])
+            if first == 0:
                 nc.sync.dma_start(out=bias_rows[0:1, :], in_=bx.rearrange("(o c) n -> o (c n)", o=1))
         h_raw = keep.tile([P, H], BF16, name="h_raw")
         nc.sync.dma_start(out=h_raw[:], in_=hidden_states)
         x_raw = []
         for part in range(QUARTERS):
             if part % 2 == 0:
-                raw = raw_pool.tile([P, 2, QUARTER_K], BF16, name="raw")
+                raw = raw_pool.tile([P, 2, QUARTER_K], BF16, name="raw", align_bytes=512)
             nc.sync.dma_start(out=raw[:, part % 2, :], in_=input_word[:, part * QUARTER_K : (part + 1) * QUARTER_K])
             x_raw.append(raw[:, part % 2 : part % 2 + 1, :])
         for n in range(RAW_TILES - 4):
             load_next()
 
-        identity = keep.tile([P, P], F32, name="identity")
+        identity = keep.tile([P, P], F32, name="identity", align_bytes=512)
         masks.make_identity(nc, identity[:])
         ones = keep.tile([P, P], BF16, name="ones")
         nc.vector.memset(ones[:], 1.0)
@@ -121,22 +123,22 @@ def tile_compute_gate_k_kernel(tc, input_word, hidden_states, Wx, bx, Wh, out_0,
         nc.vector.memset(early[:], 0.0)
         nc.scalar.activation(out=early[:], in_=early[:], func=ACT.Sigmoid)
 
-        x_codes = keep.tile([P, X_PASSES * P], U32, name="x_codes", align_bytes=64)
-        x_scales = keep.tile([P, X_PASSES * P], U8, name="x_scales", align_bytes=64)
-        h_codes = keep.tile([P, P], U32, name="h_codes", align_bytes=64)
-        h_scales = keep.tile([P, P], U8, name="h_scales", align_bytes=64)
-        wh_codes = keep.tile([P, OUT], U32, name="wh_codes", align_bytes=64)
-        wh_scales = keep.tile([P, OUT], U8, name="wh_scales", align_bytes=64)
+        x_codes = keep.tile([P, X_PASSES * P], U32, name="x_codes", align_bytes=256)
+        x_scales = keep.tile([P, X_PASSES * P], U8, name="x_scales", align_bytes=256)
+        h_codes = keep.tile([P, P], U32, name="h_codes", align_bytes=256)
+        h_scales = keep.tile([P, P], U8, name="h_scales", align_bytes=256)
+        wh_codes = keep.tile([P, OUT], U32, name="wh_codes", align_bytes=256)
+        wh_scales = keep.tile([P, OUT], U8, name="wh_scales", align_bytes=256)
         wx_codes = []
         wx_scales = []
-        bias = keep.tile([P, OUT], F32, name="bias")
+        bias = keep.tile([P, OUT], BF16, name="bias")
         results = keep.tile([P, GATES * CELLS, H], F32, name="results")
         net_sums = []
         nets = []
 
         def gather_firsts(raw, part):
             blocks = raw.shape[1]
-            firsts = firsts_pool.tile([P, blocks, (QUARTER_PASSES - STRIDED[part]) * P * 2], BF16, name="firsts")
+            firsts = firsts_pool.tile([P, blocks, (QUARTER_PASSES - STRIDED[part]) * P * 2], BF16, name="firsts", align_bytes=512)
             words = raw[:, :, STRIDED[part] * K_PASS :]
             nc.vector.tensor_copy(
                 out=firsts[:].rearrange("p k (n s i) -> p k n s i", s=2, i=RUN),
@@ -166,27 +168,27 @@ def tile_compute_gate_k_kernel(tc, input_word, hidden_states, Wx, bx, Wh, out_0,
         def quantise(grouped, codes, scales):
             nc.vector.quantize_mx(out=codes.bitcast(FP8X4), scales=scales, in_=grouped)
 
-        def transpose_bank(stationaries, grouped):
+        def transpose_bank(stationaries, grouped, vector_copies=False):
             bank = banks.tile([P, BANK_WORDS], F32, name="bank")
             for i, stationary in enumerate(stationaries):
                 nc.tensor.transpose(bank[:, i * P : (i + 1) * P], stationary, identity[:])
             width = len(stationaries) * P
             regrouped = bank[:, :width].rearrange("p (g u r i) -> p g r u i", u=2, i=2, r=P // 2)
             target = grouped.bitcast(F32).rearrange("p (g r i u) -> p g r u i", u=2, i=2, r=P // 2)
-            if counts["banks"] % VECTOR_COPY_EVERY == VECTOR_COPY_EVERY - 1:
+            if vector_copies or counts["banks"] % VECTOR_COPY_EVERY == VECTOR_COPY_EVERY - 1:
                 nc.vector.tensor_copy(out=target, in_=regrouped)
             else:
                 nc.scalar.copy(out=target, in_=regrouped)
             counts["banks"] += 1
 
-        def prepare(jobs, codes, scales, after_bank):
+        def prepare(jobs, codes, scales, after_bank, vector_banks=(), quantise_banks=QUANTISE_BANKS):
             for b, stationaries in enumerate(jobs):
                 width = BANK_WORDS * 2
-                part = b % QUANTISE_BANKS
+                part = b % quantise_banks
                 if part == 0:
-                    grouped = grouped_pool.tile([P, QUANTISE_BANKS * width], BF16, name="grouped", align_bytes=64)
-                transpose_bank(stationaries, grouped[:, part * width : (part + 1) * width])
-                if part == QUANTISE_BANKS - 1:
+                    grouped = grouped_pool.tile([P, quantise_banks * width], BF16, name="grouped", align_bytes=256)
+                transpose_bank(stationaries, grouped[:, part * width : (part + 1) * width], b in vector_banks)
+                if part == quantise_banks - 1:
                     cols = slice((b - part) * PAIR, (b + 1) * PAIR)
                     copied.append((grouped[:], codes[:, cols], scales[:, cols]))
                     if len(copied) > 1:
@@ -194,13 +196,13 @@ def tile_compute_gate_k_kernel(tc, input_word, hidden_states, Wx, bx, Wh, out_0,
                 after_bank(b)
 
         def spread_bias(j):
-            cols = slice(j * BANK_WORDS, (j + 1) * BANK_WORDS)
-            spread = banks.tile([P, BANK_WORDS], F32, name="bank")
-            nc.tensor.matmul(out=spread[:], lhsT=ones[:], rhs=bias_rows[:, cols], start=True, stop=True)
-            if j in BIAS_SCALAR:
-                nc.scalar.copy(out=bias[:, cols], in_=spread[:])
-            else:
-                nc.vector.tensor_copy(out=bias[:, cols], in_=spread[:])
+            cols = slice(j * 2 * BANK_WORDS, (j + 1) * 2 * BANK_WORDS)
+            spread = banks.tile([P, 2 * BANK_WORDS], BF16, name="bank")
+            for n in range(2):
+                half = slice(n * BANK_WORDS, (n + 1) * BANK_WORDS)
+                from_row = bias_rows[:, cols.start + half.start : cols.start + half.stop]
+                nc.tensor.matmul(out=spread[:, half], lhsT=ones[:], rhs=from_row, start=True, stop=True)
+            nc.vector.tensor_copy(out=bias[:, cols], in_=spread[:])
 
         firsts = {}
 
@@ -212,7 +214,7 @@ def tile_compute_gate_k_kernel(tc, input_word, hidden_states, Wx, bx, Wh, out_0,
                 if b == 1:
                     move_seconds(raw, n % QUARTERS)
 
-        h_grouped = keep.tile([P, H], BF16, name="h_grouped", align_bytes=64)
+        h_grouped = keep.tile([P, H], BF16, name="h_grouped", align_bytes=256)
         for half in range(2):
             cols = slice(half * OUT // 2, (half + 1) * OUT // 2)
             jobs = []
@@ -221,7 +223,7 @@ def tile_compute_gate_k_kernel(tc, input_word, hidden_states, Wx, bx, Wh, out_0,
                 jobs.append(
                     strided_windows(passes[:, b, :].bitcast(F32)) + strided_windows(passes[:, b + 1, :].bitcast(F32))
                 )
-            prepare(jobs, wh_codes[:, cols], wh_scales[:, cols], (lambda b: move(0, b - 2)) if half == 1 else (lambda b: None))
+            prepare(jobs, wh_codes[:, cols], wh_scales[:, cols], (lambda b: move(0, b - 2)) if half == 1 else (lambda b: None), WH_V)
             load_next()
             for j in BIAS_AFTER_WH[half]:
                 spread_bias(j)
@@ -285,8 +287,8 @@ def tile_compute_gate_k_kernel(tc, input_word, hidden_states, Wx, bx, Wh, out_0,
         def prepare_wx(m):
             i, part = divmod(m, QUARTERS)
             if part == 0:
-                wx_codes.append(weight_pool.tile([P, X_PASSES * PAIR], U32, name="codes", align_bytes=64))
-                wx_scales.append(weight_pool.tile([P, X_PASSES * PAIR], U8, name="scales", align_bytes=64))
+                wx_codes.append(weight_pool.tile([P, X_PASSES * PAIR], U32, name="codes", align_bytes=256))
+                wx_scales.append(weight_pool.tile([P, X_PASSES * PAIR], U8, name="scales", align_bytes=256))
             raw = wx_raw[m]
 
             def after_bank(b):
@@ -311,7 +313,10 @@ def tile_compute_gate_k_kernel(tc, input_word, hidden_states, Wx, bx, Wh, out_0,
                     windows(raw, part, firsts[QUARTERS + m], 0, g) + windows(raw, part, firsts[QUARTERS + m], 1, g)
                 )
             cols = slice(part * QUARTER_PASSES * PAIR, (part + 1) * QUARTER_PASSES * PAIR)
-            prepare(jobs, wx_codes[i][:, cols], wx_scales[i][:, cols], after_bank)
+            if m < last:
+                prepare(jobs, wx_codes[i][:, cols], wx_scales[i][:, cols], after_bank)
+            else:
+                prepare(jobs, wx_codes[i][:, cols], wx_scales[i][:, cols], after_bank, LAST_V, LAST_Q)
             load_next()
 
         for m in range(PAIRS * QUARTERS):

from contextlib import ExitStack

import concourse.masks as masks
import concourse.mybir as mybir

F32 = mybir.dt.float32
BF16 = mybir.dt.bfloat16
I32 = mybir.dt.int32
U32 = mybir.dt.uint32
U8 = mybir.dt.uint8
FP8X4 = mybir.dt.float8_e4m3fn_x4
ACT = mybir.ActivationFunctionType
ALU = mybir.AluOpType

P = 128
PACK = 4
K_PASS = P * PACK
IN = 8192
H = 512
CELLS = 2
GATES = 2
OUT = CELLS * GATES * H
X_PASSES = IN // K_PASS
BLOCKS = OUT // P
PAIR = 2 * P
PAIRS = OUT // PAIR
PAIRS_PER_GATE = H // PAIR

QUARTERS = 4
QUARTER_PASSES = X_PASSES // QUARTERS
QUARTER_K = QUARTER_PASSES * K_PASS

WORDS_PER_PASS = K_PASS // 2
BANK_WORDS = 512
BANK_PASSES = BANK_WORDS // WORDS_PER_PASS
QUANTISE_BANKS = 2
WH_PARTS = 4
RUN = 16
STRIDED = (1, 1, 1, 1)
NEAR = 4
WH_V = ()
WH_CUTS = (0, 4, 8, 12, 16)
LAST_V = (2,)
LAST_Q = 1
BIAS_AFTER_WH = ((0,), (1,))
BIAS_AFTER_X = ((), ())
BIAS_SCALAR = ()
BURST = 2
MULTIPLY_LAG = 2

VECTOR_COPY_EVERY = 14

RAW_TILES = 13
TRANSPOSE_BANKS = 6
SUM_BANKS = 2

FLOPS = 2 * P * OUT * (IN + H)


def tile_compute_gate_k_kernel(tc, input_word, hidden_states, Wx, bx, Wh, out_0, out_1):
    nc = tc.nc
    with ExitStack() as ctx:
        keep = ctx.enter_context(tc.tile_pool(name="keep", bufs=1))
        raw_pool = ctx.enter_context(tc.tile_pool(name="raw", bufs=RAW_TILES))
        firsts_pool = ctx.enter_context(tc.tile_pool(name="firsts", bufs=4))
        grouped_pool = ctx.enter_context(tc.tile_pool(name="grouped", bufs=4))
        weight_pool = ctx.enter_context(tc.tile_pool(name="weight", bufs=2))
        out_pool = ctx.enter_context(tc.tile_pool(name="out", bufs=2))
        banks = ctx.enter_context(tc.psum_pool(name="banks", bufs=TRANSPOSE_BANKS))
        sums = ctx.enter_context(tc.psum_pool(name="sums", bufs=SUM_BANKS))
        ctx.enter_context(tc.manual_schedule())

        pair_order = []
        for gate in range(GATES):
            for cell in range(CELLS):
                for part in range(PAIRS_PER_GATE):
                    pair_order.append((gate, cell, part))

        def net_columns(i):
            gate, cell, part = pair_order[i]
            first = (cell * GATES + gate) * H + part * PAIR
            return slice(first, first + PAIR)

        wx_rows = Wx.rearrange("c n k -> (c n) k")
        wx_raw = []

        def load_next():
            if len(wx_raw) < PAIRS * QUARTERS:
                i, part = divmod(len(wx_raw), QUARTERS)
                raw = raw_pool.tile([P, 2, QUARTER_K], BF16, name="raw", align_bytes=512)
                rows = wx_rows[net_columns(i), :].rearrange("(b p) k -> p b k", p=P)
                nc.sync.dma_start(out=raw[:], in_=rows[:, :, part * QUARTER_K : (part + 1) * QUARTER_K])
                wx_raw.append(raw)

        bias_rows = keep.tile([P, OUT], BF16, name="bias_rows")
        nc.vector.memset(bias_rows[:].bitcast(I32), 0)
        wh_blocks = Wh.rearrange("c (b p) k -> p (c b) k", p=P)
        wh_raw = []
        for part in range(2):
            wh_raw.append(raw_pool.tile([P, 2, QUARTER_K], BF16, name="raw", align_bytes=512))
        for first, end in zip(WH_CUTS, WH_CUTS[1:]):
            half, b = divmod(first, BLOCKS // 2)
            raw = wh_raw[half][:].rearrange("p a (b k) -> p (a b) k", k=K_PASS)
            nc.sync.dma_start(out=raw[:, b : b + end - first, :], in_=wh_blocks[:, first:end, :])
            if first == 0:
                nc.sync.dma_start(out=bias_rows[0:1, :], in_=bx.rearrange("(o c) n -> o (c n)", o=1))
        h_raw = keep.tile([P, H], BF16, name="h_raw")
        nc.sync.dma_start(out=h_raw[:], in_=hidden_states)
        x_raw = []
        for part in range(QUARTERS):
            if part % 2 == 0:
                raw = raw_pool.tile([P, 2, QUARTER_K], BF16, name="raw", align_bytes=512)
            nc.sync.dma_start(out=raw[:, part % 2, :], in_=input_word[:, part * QUARTER_K : (part + 1) * QUARTER_K])
            x_raw.append(raw[:, part % 2 : part % 2 + 1, :])
        for n in range(RAW_TILES - 4):
            load_next()

        identity = keep.tile([P, P], F32, name="identity", align_bytes=512)
        masks.make_identity(nc, identity[:])
        ones = keep.tile([P, P], BF16, name="ones")
        nc.vector.memset(ones[:], 1.0)
        early = keep.tile([P, 1], F32, name="early")
        nc.vector.memset(early[:], 0.0)
        nc.scalar.activation(out=early[:], in_=early[:], func=ACT.Sigmoid)

        x_codes = keep.tile([P, X_PASSES * P], U32, name="x_codes", align_bytes=256)
        x_scales = keep.tile([P, X_PASSES * P], U8, name="x_scales", align_bytes=256)
        h_codes = keep.tile([P, P], U32, name="h_codes", align_bytes=256)
        h_scales = keep.tile([P, P], U8, name="h_scales", align_bytes=256)
        wh_codes = keep.tile([P, OUT], U32, name="wh_codes", align_bytes=256)
        wh_scales = keep.tile([P, OUT], U8, name="wh_scales", align_bytes=256)
        wx_codes = []
        wx_scales = []
        bias = keep.tile([P, OUT], BF16, name="bias")
        results = keep.tile([P, GATES * CELLS, H], F32, name="results")
        net_sums = []
        nets = []

        def gather_firsts(raw, part):
            blocks = raw.shape[1]
            firsts = firsts_pool.tile([P, blocks, (QUARTER_PASSES - STRIDED[part]) * P * 2], BF16, name="firsts", align_bytes=512)
            words = raw[:, :, STRIDED[part] * K_PASS :]
            nc.vector.tensor_copy(
                out=firsts[:].rearrange("p k (n s i) -> p k n s i", s=2, i=RUN),
                in_=words.rearrange("p k (s n u i) -> p u k n s i", s=2, u=2, i=RUN)[:, 0],
            )
            return firsts

        def move_seconds(raw, part):
            words = raw[:, :, STRIDED[part] * K_PASS :]
            runs = words.rearrange("p k (s n u i) -> p s u k n i", s=2, u=2, i=RUN)
            nc.vector.tensor_copy(out=runs[:, 1, 0], in_=runs[:, 0, 1])

        def strided_windows(words):
            return [words[:, u::2] for u in range(2)]

        def windows(raw, part, firsts, block, g):
            words = raw[:, block, :].bitcast(F32)
            if g < STRIDED[part]:
                return strided_windows(words[:, g * WORDS_PER_PASS : (g + 1) * WORDS_PER_PASS])
            first = (g - STRIDED[part]) * P
            second = STRIDED[part] * WORDS_PER_PASS + (QUARTER_PASSES - STRIDED[part]) * P + first
            return [firsts[:, block, :].bitcast(F32)[:, first : first + P], words[:, second : second + P]]

        copied = []
        counts = {"banks": 0}

        def quantise(grouped, codes, scales):
            nc.vector.quantize_mx(out=codes.bitcast(FP8X4), scales=scales, in_=grouped)

        def transpose_bank(stationaries, grouped, vector_copies=False):
            bank = banks.tile([P, BANK_WORDS], F32, name="bank")
            for i, stationary in enumerate(stationaries):
                nc.tensor.transpose(bank[:, i * P : (i + 1) * P], stationary, identity[:])
            width = len(stationaries) * P
            regrouped = bank[:, :width].rearrange("p (g u r i) -> p g r u i", u=2, i=2, r=P // 2)
            target = grouped.bitcast(F32).rearrange("p (g r i u) -> p g r u i", u=2, i=2, r=P // 2)
            if vector_copies or counts["banks"] % VECTOR_COPY_EVERY == VECTOR_COPY_EVERY - 1:
                nc.vector.tensor_copy(out=target, in_=regrouped)
            else:
                nc.scalar.copy(out=target, in_=regrouped)
            counts["banks"] += 1

        def prepare(jobs, codes, scales, after_bank, vector_banks=(), quantise_banks=QUANTISE_BANKS):
            for b, stationaries in enumerate(jobs):
                width = BANK_WORDS * 2
                part = b % quantise_banks
                if part == 0:
                    grouped = grouped_pool.tile([P, quantise_banks * width], BF16, name="grouped", align_bytes=256)
                transpose_bank(stationaries, grouped[:, part * width : (part + 1) * width], b in vector_banks)
                if part == quantise_banks - 1:
                    cols = slice((b - part) * PAIR, (b + 1) * PAIR)
                    copied.append((grouped[:], codes[:, cols], scales[:, cols]))
                    if len(copied) > 1:
                        quantise(*copied.pop(0))
                after_bank(b)

        def spread_bias(j):
            cols = slice(j * 2 * BANK_WORDS, (j + 1) * 2 * BANK_WORDS)
            spread = banks.tile([P, 2 * BANK_WORDS], BF16, name="bank")
            for n in range(2):
                half = slice(n * BANK_WORDS, (n + 1) * BANK_WORDS)
                from_row = bias_rows[:, cols.start + half.start : cols.start + half.stop]
                nc.tensor.matmul(out=spread[:, half], lhsT=ones[:], rhs=from_row, start=True, stop=True)
            nc.vector.tensor_copy(out=bias[:, cols], in_=spread[:])

        firsts = {}

        def move(n, b):
            if n < QUARTERS + PAIRS * QUARTERS:
                raw = x_raw[n] if n < QUARTERS else wx_raw[n - QUARTERS][:]
                if b == 0:
                    firsts[n] = gather_firsts(raw, n % QUARTERS)
                if b == 1:
                    move_seconds(raw, n % QUARTERS)

        h_grouped = keep.tile([P, H], BF16, name="h_grouped", align_bytes=256)
        for half in range(2):
            cols = slice(half * OUT // 2, (half + 1) * OUT // 2)
            jobs = []
            for b in range(0, BLOCKS // 2, 2):
                passes = wh_raw[half][:].rearrange("p k (b w) -> p (k b) w", w=K_PASS)
                jobs.append(
                    strided_windows(passes[:, b, :].bitcast(F32)) + strided_windows(passes[:, b + 1, :].bitcast(F32))
                )
            prepare(jobs, wh_codes[:, cols], wh_scales[:, cols], (lambda b: move(0, b - 2)) if half == 1 else (lambda b: None), WH_V)
            load_next()
            for j in BIAS_AFTER_WH[half]:
                spread_bias(j)
            if half == 1:
                transpose_bank(strided_windows(h_raw[:].bitcast(F32)), h_grouped[:])
        quantise(h_grouped[:], h_codes[:], h_scales[:])
        for part in range(QUARTERS):
            raw = x_raw[part]
            cols = slice(part * QUARTER_PASSES * P, (part + 1) * QUARTER_PASSES * P)
            jobs = []
            for g in range(0, QUARTER_PASSES, 2):
                jobs.append(windows(raw, part, firsts[part], 0, g) + windows(raw, part, firsts[part], 0, g + 1))
            prepare(jobs, x_codes[:, cols], x_scales[:, cols], lambda b: move(part + 1, b))
            if part % 2 == 1:
                load_next()
                for j in BIAS_AFTER_X[part // 2]:
                    spread_bias(j)

        def multiply(m):
            i, part = divmod(m, QUARTERS)
            if part == 0:
                net_sums.append(sums.tile([P, BANK_WORDS], F32, name="acc"))
                nc.tensor.matmul_mx(
                    out=net_sums[i][:, :PAIR],
                    lhsT=h_codes[:].bitcast(FP8X4),
                    lhsT_scale=h_scales[:],
                    rhs=wh_codes[:, net_columns(i)].bitcast(FP8X4),
                    rhs_scale=wh_scales[:, net_columns(i)],
                    start=True,
                    stop=False,
                )
            for g in range(part * QUARTER_PASSES, (part + 1) * QUARTER_PASSES):
                x_cols = slice(g * P, (g + 1) * P)
                w_cols = slice(g * PAIR, (g + 1) * PAIR)
                nc.tensor.matmul_mx(
                    out=net_sums[i][:, :PAIR],
                    lhsT=x_codes[:, x_cols].bitcast(FP8X4),
                    lhsT_scale=x_scales[:, x_cols],
                    rhs=wx_codes[i][:, w_cols].bitcast(FP8X4),
                    rhs_scale=wx_scales[i][:, w_cols],
                    start=False,
                    stop=(g == X_PASSES - 1),
                )

        def add_bias(i):
            net = out_pool.tile([P, PAIR], F32, name="net")
            nc.vector.tensor_tensor(out=net[:], in0=net_sums[i][:, :PAIR], in1=bias[:, net_columns(i)], op=ALU.add)
            nets.append(net)

        def activate(i):
            gate, cell, part = pair_order[i]
            nc.scalar.activation(
                out=results[:, i // PAIRS_PER_GATE, part * PAIR : (part + 1) * PAIR],
                in_=nets[i][:],
                func=ACT.Sigmoid if gate == 0 else ACT.Tanh,
            )

        last = PAIRS * QUARTERS - 1
        ended = [0, 0, 0]

        def prepare_wx(m):
            i, part = divmod(m, QUARTERS)
            if part == 0:
                wx_codes.append(weight_pool.tile([P, X_PASSES * PAIR], U32, name="codes", align_bytes=256))
                wx_scales.append(weight_pool.tile([P, X_PASSES * PAIR], U8, name="scales", align_bytes=256))
            raw = wx_raw[m]

            def after_bank(b):
                if m < NEAR:
                    move(QUARTERS + m + 1, b)
                if m >= NEAR - 1:
                    move(QUARTERS + m + 2, b - 2)
                if b == 1 and ended[1] < ended[0] // QUARTERS:
                    add_bias(ended[1])
                    ended[1] += 1
                if b == 3 and ended[2] < ended[1]:
                    activate(ended[2])
                    ended[2] += 1
                if b == 3 and m >= MULTIPLY_LAG and (m - MULTIPLY_LAG) % BURST == BURST - 1:
                    while ended[0] <= m - MULTIPLY_LAG:
                        multiply(ended[0])
                        ended[0] += 1

            jobs = []
            for g in range(QUARTER_PASSES):
                jobs.append(
                    windows(raw, part, firsts[QUARTERS + m], 0, g) + windows(raw, part, firsts[QUARTERS + m], 1, g)
                )
            cols = slice(part * QUARTER_PASSES * PAIR, (part + 1) * QUARTER_PASSES * PAIR)
            if m < last:
                prepare(jobs, wx_codes[i][:, cols], wx_scales[i][:, cols], after_bank)
            else:
                prepare(jobs, wx_codes[i][:, cols], wx_scales[i][:, cols], after_bank, LAST_V, LAST_Q)
            load_next()

        for m in range(PAIRS * QUARTERS):
            prepare_wx(m)
        quantise(*copied.pop(0))
        for m in range(ended[0], last + 1):
            multiply(m)
        add_bias(PAIRS - 1)
        activate(PAIRS - 1)

        for i in range(0, PAIRS, PAIRS_PER_GATE):
            gate, cell, part = pair_order[i]
            out = out_1 if gate == 0 else out_0
            cuts = (0, H) if i + PAIRS_PER_GATE < PAIRS else (0, H - PAIR, H)
            for first, end in zip(cuts, cuts[1:]):
                nc.sync.dma_start(
                    out=out[:, cell, first:end], in_=results[:, i // PAIRS_PER_GATE, first:end]
                )
